import numpy as np
import ml_dtypes


def mxq(x, axis, fmt="e4m3"):
    dtype, down = {"e4m3": (ml_dtypes.float8_e4m3fn, 7), "e5m2": (ml_dtypes.float8_e5m2, 14)}[fmt]
    v = np.moveaxis(np.asarray(x, np.float32).astype(ml_dtypes.bfloat16).astype(np.float64), axis, -1)
    blocks = v.reshape(v.shape[:-1] + (-1, 32))
    amax = np.abs(blocks).max(-1, keepdims=True)
    byte = np.maximum(np.where(amax > 0, np.frexp(amax)[1] - 1 + 127, 0) - down, 1)
    scale = np.exp2(byte - 127.0)
    codes = (blocks / scale).astype(np.float32).astype(dtype).astype(np.float64)
    return np.moveaxis((codes * scale).reshape(v.shape), -1, axis)


WIDE = False


def mx_kscale(k):
    if not WIDE:
        return np.ones(k)
    levels = np.array([10, -10, 5, -5, 0])
    a = np.random.permutation(np.resize(levels, k // 512 * 4)).reshape(k // 512, 4)
    idx = np.arange(k)
    return np.exp2(a[idx // 512, idx % 128 // 32])


BF16 = ml_dtypes.bfloat16


def bf(x):
    return np.asarray(x, np.float32).astype(BF16)


def f64(x):
    return np.asarray(x).astype(np.float64)


B, N, C, H, D = 8, 1024, 1024, 4, 32
EPS = 1e-12
SCALE = float(D) ** 0.25
VG = 4.0


def normalize(t):
    n = np.sqrt((t * t).sum(-1, keepdims=True))
    return t / np.maximum(n, EPS)


def heads(t):
    return t.reshape(B, N, H, D).transpose(0, 2, 1, 3)


def setup_inputs():
    s = mx_kscale(C)
    return {'x': bf(np.random.standard_normal((B, N, C)) * s),
            'Wk': bf(np.random.standard_normal((H * D, C)) / np.sqrt(C) / s),
            'bk': bf(np.random.standard_normal(H * D) * 0.1),
            'Wv': bf(np.random.standard_normal((H * D, C)) * VG / np.sqrt(C) / s),
            'bv': bf(np.random.standard_normal(H * D) * 0.1)}


def reference(x, Wk, bk, Wv, bv):
    xq = mxq(f64(x), 2, 'e4m3')
    k = heads((xq @ mxq(f64(Wk), 1, 'e4m3').T) + f64(bk))
    v = heads((xq @ mxq(f64(Wv), 1, 'e4m3').T) + f64(bv))
    kn = normalize(k) * SCALE
    vN = v / N
    kk = (kn[..., :, None] * kn[..., None, :]).reshape(B, H, N, D * D)
    vq = mxq(vN, 2, 'e4m3')
    mod_v = mxq(kk, 2, 'e4m3').transpose(0, 1, 3, 2) @ vq
    mod_n = kk.sum(2) / N
    kv_mod = np.concatenate([mod_n[..., None], mod_v], axis=-1).reshape(B, H, D, D, D + 1)
    kv_v = mxq(kn, 2, 'e4m3').transpose(0, 1, 3, 2) @ vq
    kv_n = kn.sum(2) / N
    kv = np.concatenate([kv_n[..., None], kv_v], axis=-1)
    vsum = np.concatenate([np.ones((B, H, 1)), vN.sum(2)], axis=-1)[:, :, None, :]
    return kv_mod, kv, vsum

@@ -1,0 +1,319 @@
+from contextlib import ExitStack
+
+import concourse.mybir as mybir
+from concourse.masks import make_identity
+
+F32 = mybir.dt.float32
+BF16 = mybir.dt.bfloat16
+U32 = mybir.dt.uint32
+U8 = mybir.dt.uint8
+FP8X4 = mybir.dt.float8_e4m3fn_x4
+ACT = mybir.ActivationFunctionType
+ALU = mybir.AluOpType
+
+P = 128
+B = 8
+N_TOK = 1024
+C = 1024
+H = 4
+D = 32
+PACK = 4
+K_PASS = P * PACK
+GROUPS = B * N_TOK // K_PASS
+HALF = D // 2
+N_DIAG = HALF + 1
+D_EXT = D + HALF
+N_BLOCKS = N_DIAG + 1
+A_PITCH = D_EXT
+EPS = 1e-12
+SCALE = 32.0 ** 0.25
+GP_DIAGS = 0
+
+FLOPS = 2 * B * N_TOK * C * 2 * H * D + 2 * B * H * N_TOK * (D * D + D) * D
+
+
+def tile_taylorsoftmaxattention_pa_t_kernel(tc, x, Wk, bk, Wv, bv, out_0, out_1, out_2):
+    nc = tc.nc
+    with ExitStack() as ctx:
+        const = ctx.enter_context(tc.tile_pool(name="const", bufs=1))
+        xpool = ctx.enter_context(tc.tile_pool(name="xpool", bufs=3))
+        work = ctx.enter_context(tc.tile_pool(name="work", bufs=2))
+        keep = ctx.enter_context(tc.tile_pool(name="keep", bufs=4))
+        ps_xt = ctx.enter_context(tc.psum_pool(name="ps_xt", bufs=2))
+        ps_s1 = ctx.enter_context(tc.psum_pool(name="ps_s1", bufs=2))
+        ps_kn = ctx.enter_context(tc.psum_pool(name="ps_kn", bufs=2))
+        ps_misc = ctx.enter_context(tc.psum_pool(name="ps_misc", bufs=2))
+
+        w_sb = const.tile([P, 2, C], BF16, name="w_sb")
+        nc.scalar.dma_start(out=w_sb[:, 0, :], in_=Wk)
+        nc.scalar.dma_start(out=w_sb[:, 1, :], in_=Wv)
+        ident = const.tile([P, P], F32, name="ident")
+        make_identity(nc, ident[:])
+        same_head = const.tile([P, P], F32, name="same_head")
+        nc.vector.memset(same_head[:], 0.0)
+        for h in range(H):
+            nc.vector.memset(same_head[D * h : D * h + D, D * h : D * h + D], 1.0)
+
+        brow = const.tile([P, P], BF16, name="brow")
+        nc.vector.memset(brow[:], 0.0)
+        nc.scalar.dma_start(out=brow[0:1, :], in_=bk.rearrange("(o f) -> o f", o=1))
+        nc.scalar.dma_start(out=brow[1:2, :], in_=bv.rearrange("(o f) -> o f", o=1))
+        brow_f = const.tile([P, P], F32, name="brow_f")
+        nc.vector.tensor_copy(out=brow_f[:], in_=brow[:])
+        bcol_ps = ps_misc.tile([P, P], F32, name="bcol_ps", tag="misc")
+        nc.tensor.transpose(out=bcol_ps[:], in_=brow_f[:], identity=ident[:])
+        bias = const.tile([P, 2], F32, name="bias")
+        nc.vector.tensor_copy(out=bias[:, 0:1], in_=bcol_ps[:, 0:1])
+        nc.vector.tensor_scalar(
+            out=bias[:, 1:2], in0=bcol_ps[:, 1:2], scalar1=1.0 / N_TOK, scalar2=None, op0=ALU.mult
+        )
+
+        wg = const.tile([P, 2 * 2 * P * PACK], BF16, name="wg", align_bytes=64)
+        wg_f = wg[:].bitcast(F32).rearrange("p (g n u) -> p g n u", g=2, u=2)
+        for g2 in range(2):
+            wt = ps_xt.tile([P, 2, 2 * P], F32, name="wt", tag="xt")
+            for u in range(2):
+                for kv in range(2):
+                    wb = 2 * g2 + u
+                    nc.tensor.transpose(
+                        out=wt[:, u, P * kv : P * kv + P],
+                        in_=w_sb[:, kv, :].bitcast(F32)[:, P * wb : P * wb + P],
+                        identity=ident[:],
+                    )
+            nc.vector.tensor_copy(out=wg_f[:, g2, :, :], in_=wt[:].rearrange("p u n -> p n u"))
+        w_codes = const.tile([P, 2 * 2 * P], U32, name="w_codes", align_bytes=64)
+        w_scales = const.tile([P, 2 * 2 * P], U8, name="w_scales", align_bytes=64)
+        nc.vector.quantize_mx(out=w_codes[:].bitcast(FP8X4), scales=w_scales[:], in_=wg[:])
+
+        knp = [const.tile([P, PACK, P + 4], F32, name="knp%d" % i) for i in range(4)]
+        for t in knp:
+            nc.vector.memset(t[:, :, P : P + 1], 1.0)
+        a_mat = [const.tile([P, D * (A_PITCH + 1)], F32, name="a_mat%d" % i) for i in range(2)]
+        for t in a_mat:
+            nc.vector.memset(t[:], 0.0)
+        vs_cols = const.tile([P, GROUPS], F32, name="vs_cols")
+
+        state = {}
+
+        def front(g):
+            b, gl = divmod(g, 2)
+            x_sb = xpool.tile([P, PACK, C], BF16, name="x_sb")
+            nc.sync.dma_start(
+                out=x_sb[:],
+                in_=x[b, K_PASS * gl : K_PASS * gl + K_PASS, :].rearrange("(p t) c -> p t c", t=PACK),
+            )
+            xg = work.tile([P, 2 * K_PASS * PACK], BF16, name="xg", align_bytes=64)
+            xg_f = xg[:].bitcast(F32).rearrange("p (g n u) -> p g n u", g=2, u=2)
+            for g2 in range(2):
+                for th in range(2):
+                    xt = ps_xt.tile([P, 2, 2 * P], F32, name="xt", tag="xt")
+                    for u in range(2):
+                        for tl in range(2):
+                            wb = 2 * g2 + u
+                            nc.tensor.transpose(
+                                out=xt[:, u, P * tl : P * tl + P],
+                                in_=x_sb[:, 2 * th + tl, :].bitcast(F32)[:, P * wb : P * wb + P],
+                                identity=ident[:],
+                            )
+                    nc.scalar.copy(
+                        out=xg_f[:, g2, 2 * P * th : 2 * P * th + 2 * P, :],
+                        in_=xt[:].rearrange("p u n -> p n u"),
+                    )
+            x_codes = work.tile([P, 2 * K_PASS], U32, name="x_codes", align_bytes=64)
+            x_scales = work.tile([P, 2 * K_PASS], U8, name="x_scales", align_bytes=64)
+            nc.vector.quantize_mx(out=x_codes[:].bitcast(FP8X4), scales=x_scales[:], in_=xg[:])
+
+            proj = []
+            for kv in range(2):
+                acc = ps_s1.tile([P, K_PASS], F32, name="acc", tag="s1")
+                for g2 in range(2):
+                    wcols = slice(P * (2 * g2 + kv), P * (2 * g2 + kv) + P)
+                    xcols = slice(K_PASS * g2, K_PASS * g2 + K_PASS)
+                    nc.tensor.matmul_mx(
+                        out=acc[:],
+                        lhsT=w_codes[:, wcols].bitcast(FP8X4),
+                        lhsT_scale=w_scales[:, wcols],
+                        rhs=x_codes[:, xcols].bitcast(FP8X4),
+                        rhs_scale=x_scales[:, xcols],
+                        start=(g2 == 0),
+                        stop=(g2 == 1),
+                    )
+                proj.append(acc)
+            kT = work.tile([P, K_PASS], F32, name="kT")
+            sqT = work.tile([P, K_PASS], F32, name="sqT")
+            vT = work.tile([P, K_PASS], F32, name="vT")
+            nc.scalar.activation(out=sqT[:], in_=proj[0][:], func=ACT.Square, bias=bias[:, 0:1], scale=1.0)
+            nc.scalar.activation(out=kT[:], in_=proj[0][:], func=ACT.Identity, bias=bias[:, 0:1], scale=1.0)
+            ssT = ps_s1.tile([P, K_PASS], F32, name="ssT", tag="s1")
+            nc.tensor.matmul(out=ssT[:], lhsT=same_head[:], rhs=sqT[:], start=True, stop=True)
+            rT = work.tile([P, K_PASS], F32, name="rT")
+            nc.scalar.activation(out=rT[:], in_=ssT[:], func=ACT.Abs_reciprocal_sqrt, scale=1.0 / (SCALE * SCALE))
+            nc.scalar.activation(
+                out=vT[:],
+                in_=proj[1][:],
+                func=ACT.Identity,
+                bias=bias[:, 1:2],
+                scale=1.0 / N_TOK,
+                accum_out=vs_cols[:, g : g + 1],
+            )
+            knT = work.tile([P, K_PASS], F32, name="knT")
+            nc.vector.scalar_tensor_tensor(
+                out=knT[:], in0=rT[:], scalar=SCALE / EPS, in1=kT[:], op0=ALU.min, op1=ALU.mult
+            )
+            kn_tok = ps_kn.tile([P, PACK, P], F32, name="kn_tok", tag="kn")
+            v_tok = ps_misc.tile([P, PACK, P], F32, name="v_tok", tag="misc")
+            for t in range(PACK):
+                nc.tensor.transpose(out=kn_tok[:, t, :], in_=knT[:, P * t : P * t + P], identity=ident[:])
+            for t in range(PACK):
+                nc.tensor.transpose(out=v_tok[:, t, :], in_=vT[:, P * t : P * t + P], identity=ident[:])
+
+            kx = work.tile([P, H, D_EXT, PACK], F32, name="kx")
+            nc.scalar.copy(out=kx[:, :, 0:D, :], in_=kn_tok[:].rearrange("p t (h d) -> p h d t", h=H))
+            nc.scalar.copy(out=kx[:, :, D:D_EXT, :], in_=kx[:, :, 0:HALF, :])
+            kk = work.tile([P, N_BLOCKS, K_PASS], BF16, name="kk", align_bytes=64)
+            kx_flat = kx[:, :, 0:D, :].rearrange("p h d t -> p h (d t)")
+            nc.scalar.activation(
+                out=kk[:, 0, :].rearrange("p (h n) -> p h n", h=H), in_=kx_flat, func=ACT.Square
+            )
+            nc.scalar.copy(out=kk[:, N_DIAG, :].rearrange("p (h n) -> p h n", h=H), in_=kx_flat)
+            nc.scalar.copy(
+                out=knp[g % 4][:, :, 0:P].rearrange("p t (h d) -> p t h d", h=H),
+                in_=kx[:, :, 0:D, :].rearrange("p h d t -> p t h d"),
+            )
+            vb = work.tile([P, K_PASS], BF16, name="vb", align_bytes=64)
+            nc.scalar.copy(
+                out=vb[:].rearrange("p (f t) -> p f t", t=PACK), in_=v_tok[:].rearrange("p t f -> p f t")
+            )
+            v_codes = keep.tile([P, P], U32, name="v_codes", align_bytes=64)
+            v_scales = keep.tile([P, P], U8, name="v_scales", align_bytes=64)
+            nc.vector.quantize_mx(out=v_codes[:].bitcast(FP8X4), scales=v_scales[:], in_=vb[:])
+            state[("kn_tok", g)] = kn_tok
+            state[("kx", g)] = kx
+            state[("kk", g)] = kk
+            state[("v", g)] = (v_codes, v_scales)
+
+        def products(g):
+            kn_tok = state[("kn_tok", g)]
+            kx = state[("kx", g)]
+            kk = state[("kk", g)]
+            kk_codes = keep.tile([P, N_BLOCKS * P], U32, name="kk_codes", align_bytes=64)
+            kk_scales = keep.tile([P, N_BLOCKS * P], U8, name="kk_scales", align_bytes=64)
+
+            def quantise(lo, hi):
+                nc.vector.quantize_mx(
+                    out=kk_codes[:, P * lo : P * hi].bitcast(FP8X4),
+                    scales=kk_scales[:, P * lo : P * hi],
+                    in_=kk[:, lo:hi, :].rearrange("p a n -> p (a n)"),
+                )
+
+            for dd in range(HALF - GP_DIAGS + 1, HALF + 1):
+                nc.gpsimd.tensor_tensor(
+                    out=kk[:, dd, :].rearrange("p (h n) -> p h n", h=H),
+                    in0=kx[:, :, 0:D, :].rearrange("p h d t -> p h (d t)"),
+                    in1=kx[:, :, dd : dd + D, :].rearrange("p h d t -> p h (d t)"),
+                    op=ALU.mult,
+                )
+            for dd in range(1, HALF - GP_DIAGS + 1):
+                nc.vector.tensor_tensor(
+                    out=kk[:, dd, :].rearrange("p (h d t) -> p h d t", h=H, t=PACK),
+                    in0=kn_tok[:].rearrange("p t (h d) -> p h d t", h=H),
+                    in1=kx[:, :, dd : dd + D, :],
+                    op=ALU.mult,
+                )
+                if dd == 8:
+                    quantise(0, 8)
+            quantise(8, 16)
+            quantise(16, 18)
+            state[("kkq", g)] = (kk_codes, kk_scales)
+
+        def moments(b):
+            u_sb = work.tile([P, N_BLOCKS, D], F32, name="u_sb", align_bytes=64)
+            for w in range(5):
+                n = min(4, N_BLOCKS - 4 * w) * P
+                acc2 = ps_misc.tile([P, K_PASS], F32, name="acc2", tag="misc")
+                for j in range(2):
+                    v_codes, v_scales = state[("v", 2 * b + j)]
+                    kk_codes, kk_scales = state[("kkq", 2 * b + j)]
+                    cols = slice(K_PASS * w, K_PASS * w + n)
+                    nc.tensor.matmul_mx(
+                        out=acc2[:, 0:n],
+                        lhsT=v_codes[:].bitcast(FP8X4),
+                        lhsT_scale=v_scales[:],
+                        rhs=kk_codes[:, cols].bitcast(FP8X4),
+                        rhs_scale=kk_scales[:, cols],
+                        start=(j == 0),
+                        stop=(j == 1),
+                    )
+                for h in range(H):
+                    rows = slice(D * h, D * h + D)
+                    nc.scalar.copy(
+                        out=u_sb[rows, 4 * w : 4 * w + n // P, :],
+                        in_=acc2[rows, 0:n].rearrange("p (a k i) -> p a k i", k=H, i=D)[:, :, h, :],
+                    )
+            a_flat = a_mat[b % 2]
+            a_skew = a_flat[:].rearrange("p (i q) -> p i q", q=A_PITCH + 1)
+            a_rows = a_flat[:, 0 : D * A_PITCH].rearrange("p (r c) -> p r c", c=A_PITCH)
+            u_id = u_sb[:].rearrange("p a i -> p i a")
+            nc.scalar.mul(out=a_skew[:, :, 0:1], in_=u_id[:, :, 0:1], mul=0.5)
+            nc.scalar.copy(out=a_skew[:, :, 1:HALF], in_=u_id[:, :, 1:HALF])
+            nc.scalar.copy(out=a_skew[:, 0:HALF, HALF : HALF + 1], in_=u_id[:, 0:HALF, HALF : HALF + 1])
+            nc.scalar.copy(out=a_rows[:, HALF:D, 0:HALF], in_=a_rows[:, HALF:D, D:D_EXT])
+
+            sym = work.tile([P, D * D], F32, name="sym", align_bytes=64)
+            nc.vector.tensor_tensor(
+                out=sym[:].rearrange("p (r c) -> p r c", c=D),
+                in0=a_rows[:, :, 0:D],
+                in1=a_rows[:, :, 0:D].rearrange("p r c -> p c r"),
+                op=ALU.add,
+            )
+            turned = work.tile([P, D * D], F32, name="turned", align_bytes=64)
+            nc.vector.transpose(out=turned[:], in_=sym[:])
+            kv_turned = work.tile([P, D], F32, name="kv_turned", align_bytes=64)
+            nc.vector.transpose(out=kv_turned[:], in_=u_sb[:, N_DIAG, :])
+
+            gram = ps_misc.tile([P, P + 1], F32, name="gram", tag="misc")
+            for j in range(2):
+                for t in range(PACK):
+                    kn = knp[(2 * b + j) % 4]
+                    nc.tensor.matmul(
+                        out=gram[:],
+                        lhsT=kn[:, t, 0:P],
+                        rhs=kn[:, t, 0 : P + 1],
+                        start=(j == 0 and t == 0),
+                        stop=(j == 1 and t == PACK - 1),
+                    )
+            fin = work.tile([P, D, D + 1], F32, name="fin")
+            kvf = work.tile([P, D + 1], F32, name="kvf")
+            for h in range(H):
+                rows = slice(D * h, D * h + D)
+                nc.scalar.mul(
+                    out=fin[rows, :, 0:1], in_=gram[rows, D * h : D * h + D].unsqueeze(2), mul=1.0 / N_TOK
+                )
+            nc.scalar.mul(out=kvf[:, 0:1], in_=gram[:, P : P + 1], mul=1.0 / N_TOK)
+            nc.scalar.copy(out=fin[:, :, 1 : D + 1], in_=turned[:].rearrange("p (j e) -> p j e", e=D))
+            nc.scalar.copy(out=kvf[:, 1 : D + 1], in_=kv_turned[:])
+            nc.scalar.dma_start(
+                out=out_0[b].rearrange("h i j e -> (h i) (j e)"), in_=fin[:].rearrange("p j e -> p (j e)")
+            )
+            nc.scalar.dma_start(out=out_1[b].rearrange("h d e -> (h d) e"), in_=kvf[:])
+
+        front(0)
+        for g in range(GROUPS):
+            if g + 1 < GROUPS:
+                front(g + 1)
+            products(g)
+            if g % 2 == 1:
+                moments(g // 2)
+
+        vs_pad = const.tile([P, P], F32, name="vs_pad")
+        nc.vector.memset(vs_pad[:], 0.0)
+        vs_pairs = vs_cols[:].rearrange("p (b j) -> p b j", j=2)
+        nc.vector.tensor_tensor(out=vs_pad[:, 0:B], in0=vs_pairs[:, :, 0], in1=vs_pairs[:, :, 1], op=ALU.add)
+        vs_ps = ps_misc.tile([P, P], F32, name="vs_ps", tag="misc")
+        nc.tensor.transpose(out=vs_ps[:], in_=vs_pad[:], identity=ident[:])
+        vs_fin = const.tile([P, H, D + 1], F32, name="vs_fin")
+        nc.vector.memset(vs_fin[:], 1.0)
+        nc.vector.tensor_copy(out=vs_fin[:, :, 1 : D + 1], in_=vs_ps[:].rearrange("p (h e) -> p h e", h=H))
+        nc.sync.dma_start(
+            out=out_2.rearrange("b h o e -> b (h o e)"), in_=vs_fin[0:B, :, :].rearrange("p h e -> p (h e)")
+        )

@@ -27,7 +27,7 @@ N_BLOCKS = N_DIAG + 1
 A_PITCH = D_EXT
 EPS = 1e-12
 SCALE = 32.0 ** 0.25
-GP_DIAGS = 0
+GP_DIAGS = 5
 
 FLOPS = 2 * B * N_TOK * C * 2 * H * D + 2 * B * H * N_TOK * (D * D + D) * D
 

@@ -28,6 +28,8 @@ A_PITCH = D_EXT
 EPS = 1e-12
 SCALE = 32.0 ** 0.25
 GP_DIAGS = 5
+V_DIAGS = N_DIAG - GP_DIAGS
+WINDOWS_EARLY = 3
 
 FLOPS = 2 * B * N_TOK * C * 2 * H * D + 2 * B * H * N_TOK * (D * D + D) * D
 
@@ -44,29 +46,32 @@ def tile_taylorsoftmaxattention_pa_t_kernel(tc, x, Wk, bk, Wv, bv, out_0, out_1,
         ps_kn = ctx.enter_context(tc.psum_pool(name="ps_kn", bufs=2))
         ps_misc = ctx.enter_context(tc.psum_pool(name="ps_misc", bufs=2))
 
+        state = {}
+
+        def load_x(g):
+            b, gl = divmod(g, 2)
+            x_sb = xpool.tile([P, PACK, C], BF16, name="x_sb")
+            nc.sync.dma_start(
+                out=x_sb[:],
+                in_=x[b, K_PASS * gl : K_PASS * gl + K_PASS, :].rearrange("(p t) c -> p t c", t=PACK),
+            )
+            state[("x_sb", g)] = x_sb
+
         w_sb = const.tile([P, 2, C], BF16, name="w_sb")
-        nc.scalar.dma_start(out=w_sb[:, 0, :], in_=Wk)
-        nc.scalar.dma_start(out=w_sb[:, 1, :], in_=Wv)
+        nc.sync.dma_start(out=w_sb[:, 0, :], in_=Wk)
+        nc.sync.dma_start(out=w_sb[:, 1, :], in_=Wv)
+        brow = const.tile([P, P], BF16, name="brow")
+        nc.vector.memset(brow[:], 0.0)
+        nc.sync.dma_start(out=brow[0:1, :], in_=bk.rearrange("(o f) -> o f", o=1))
+        nc.sync.dma_start(out=brow[1:2, :], in_=bv.rearrange("(o f) -> o f", o=1))
+        for g in range(3):
+            load_x(g)
         ident = const.tile([P, P], F32, name="ident")
         make_identity(nc, ident[:])
         same_head = const.tile([P, P], F32, name="same_head")
         nc.vector.memset(same_head[:], 0.0)
         for h in range(H):
             nc.vector.memset(same_head[D * h : D * h + D, D * h : D * h + D], 1.0)
-
-        brow = const.tile([P, P], BF16, name="brow")
-        nc.vector.memset(brow[:], 0.0)
-        nc.scalar.dma_start(out=brow[0:1, :], in_=bk.rearrange("(o f) -> o f", o=1))
-        nc.scalar.dma_start(out=brow[1:2, :], in_=bv.rearrange("(o f) -> o f", o=1))
-        brow_f = const.tile([P, P], F32, name="brow_f")
-        nc.vector.tensor_copy(out=brow_f[:], in_=brow[:])
-        bcol_ps = ps_misc.tile([P, P], F32, name="bcol_ps", tag="misc")
-        nc.tensor.transpose(out=bcol_ps[:], in_=brow_f[:], identity=ident[:])
-        bias = const.tile([P, 2], F32, name="bias")
-        nc.vector.tensor_copy(out=bias[:, 0:1], in_=bcol_ps[:, 0:1])
-        nc.vector.tensor_scalar(
-            out=bias[:, 1:2], in0=bcol_ps[:, 1:2], scalar1=1.0 / N_TOK, scalar2=None, op0=ALU.mult
-        )
 
         wg = const.tile([P, 2 * 2 * P * PACK], BF16, name="wg", align_bytes=64)
         wg_f = wg[:].bitcast(F32).rearrange("p (g n u) -> p g n u", g=2, u=2)
@@ -85,6 +90,16 @@ def tile_taylorsoftmaxattention_pa_t_kernel(tc, x, Wk, bk, Wv, bv, out_0, out_1,
         w_scales = const.tile([P, 2 * 2 * P], U8, name="w_scales", align_bytes=64)
         nc.vector.quantize_mx(out=w_codes[:].bitcast(FP8X4), scales=w_scales[:], in_=wg[:])
 
+        brow_f = const.tile([P, P], F32, name="brow_f")
+        nc.vector.tensor_copy(out=brow_f[:], in_=brow[:])
+        bcol_ps = ps_misc.tile([P, P], F32, name="bcol_ps", tag="misc")
+        nc.tensor.transpose(out=bcol_ps[:], in_=brow_f[:], identity=ident[:])
+        bias = const.tile([P, 2], F32, name="bias")
+        nc.vector.tensor_copy(out=bias[:, 0:1], in_=bcol_ps[:, 0:1])
+        nc.vector.tensor_scalar(
+            out=bias[:, 1:2], in0=bcol_ps[:, 1:2], scalar1=1.0 / N_TOK, scalar2=None, op0=ALU.mult
+        )
+
         knp = [const.tile([P, PACK, P + 4], F32, name="knp%d" % i) for i in range(4)]
         for t in knp:
             nc.vector.memset(t[:, :, P : P + 1], 1.0)
@@ -92,16 +107,13 @@ def tile_taylorsoftmaxattention_pa_t_kernel(tc, x, Wk, bk, Wv, bv, out_0, out_1,
         for t in a_mat:
             nc.vector.memset(t[:], 0.0)
         vs_cols = const.tile([P, GROUPS], F32, name="vs_cols")
+        vs_pad = const.tile([P, P], F32, name="vs_pad")
+        nc.vector.memset(vs_pad[:], 0.0)
+        vs_fin = const.tile([P, H, D + 1], F32, name="vs_fin")
+        nc.vector.memset(vs_fin[:], 1.0)
 
-        state = {}
-
-        def front(g):
-            b, gl = divmod(g, 2)
-            x_sb = xpool.tile([P, PACK, C], BF16, name="x_sb")
-            nc.sync.dma_start(
-                out=x_sb[:],
-                in_=x[b, K_PASS * gl : K_PASS * gl + K_PASS, :].rearrange("(p t) c -> p t c", t=PACK),
-            )
+        def turn_x(g):
+            x_sb = state[("x_sb", g)]
             xg = work.tile([P, 2 * K_PASS * PACK], BF16, name="xg", align_bytes=64)
             xg_f = xg[:].bitcast(F32).rearrange("p (g n u) -> p g n u", g=2, u=2)
             for g2 in range(2):
@@ -119,10 +131,16 @@ def tile_taylorsoftmaxattention_pa_t_kernel(tc, x, Wk, bk, Wv, bv, out_0, out_1,
                         out=xg_f[:, g2, 2 * P * th : 2 * P * th + 2 * P, :],
                         in_=xt[:].rearrange("p u n -> p n u"),
                     )
+            state[("xg", g)] = xg
+
+        def quant_x(g):
             x_codes = work.tile([P, 2 * K_PASS], U32, name="x_codes", align_bytes=64)
             x_scales = work.tile([P, 2 * K_PASS], U8, name="x_scales", align_bytes=64)
-            nc.vector.quantize_mx(out=x_codes[:].bitcast(FP8X4), scales=x_scales[:], in_=xg[:])
+            nc.vector.quantize_mx(out=x_codes[:].bitcast(FP8X4), scales=x_scales[:], in_=state[("xg", g)][:])
+            state[("xq", g)] = (x_codes, x_scales)
 
+        def project_a(g):
+            x_codes, x_scales = state[("xq", g)]
             proj = []
             for kv in range(2):
                 acc = ps_s1.tile([P, K_PASS], F32, name="acc", tag="s1")
@@ -141,41 +159,59 @@ def tile_taylorsoftmaxattention_pa_t_kernel(tc, x, Wk, bk, Wv, bv, out_0, out_1,
                 proj.append(acc)
             kT = work.tile([P, K_PASS], F32, name="kT")
             sqT = work.tile([P, K_PASS], F32, name="sqT")
-            vT = work.tile([P, K_PASS], F32, name="vT")
             nc.scalar.activation(out=sqT[:], in_=proj[0][:], func=ACT.Square, bias=bias[:, 0:1], scale=1.0)
             nc.scalar.activation(out=kT[:], in_=proj[0][:], func=ACT.Identity, bias=bias[:, 0:1], scale=1.0)
             ssT = ps_s1.tile([P, K_PASS], F32, name="ssT", tag="s1")
             nc.tensor.matmul(out=ssT[:], lhsT=same_head[:], rhs=sqT[:], start=True, stop=True)
-            rT = work.tile([P, K_PASS], F32, name="rT")
-            nc.scalar.activation(out=rT[:], in_=ssT[:], func=ACT.Abs_reciprocal_sqrt, scale=1.0 / (SCALE * SCALE))
+            state[("proj", g)] = (proj[1], kT, ssT)
+
+        def project_b(g):
+            acc_v, kT, ssT = state[("proj", g)]
+            vT = work.tile([P, K_PASS], F32, name="vT")
             nc.scalar.activation(
                 out=vT[:],
-                in_=proj[1][:],
+                in_=acc_v[:],
                 func=ACT.Identity,
                 bias=bias[:, 1:2],
                 scale=1.0 / N_TOK,
                 accum_out=vs_cols[:, g : g + 1],
             )
+            rT = work.tile([P, K_PASS], F32, name="rT")
+            nc.scalar.activation(out=rT[:], in_=ssT[:], func=ACT.Abs_reciprocal_sqrt, scale=1.0 / (SCALE * SCALE))
+            state[("kr", g)] = (kT, rT)
+            state[("vT", g)] = vT
+
+        def norm_k(g):
+            kT, rT = state[("kr", g)]
             knT = work.tile([P, K_PASS], F32, name="knT")
             nc.vector.scalar_tensor_tensor(
                 out=knT[:], in0=rT[:], scalar=SCALE / EPS, in1=kT[:], op0=ALU.min, op1=ALU.mult
             )
+            state[("knT", g)] = knT
+
+        def back_a(g):
+            knT = state[("knT", g)]
             kn_tok = ps_kn.tile([P, PACK, P], F32, name="kn_tok", tag="kn")
-            v_tok = ps_misc.tile([P, PACK, P], F32, name="v_tok", tag="misc")
             for t in range(PACK):
                 nc.tensor.transpose(out=kn_tok[:, t, :], in_=knT[:, P * t : P * t + P], identity=ident[:])
-            for t in range(PACK):
-                nc.tensor.transpose(out=v_tok[:, t, :], in_=vT[:, P * t : P * t + P], identity=ident[:])
-
             kx = work.tile([P, H, D_EXT, PACK], F32, name="kx")
             nc.scalar.copy(out=kx[:, :, 0:D, :], in_=kn_tok[:].rearrange("p t (h d) -> p h d t", h=H))
             nc.scalar.copy(out=kx[:, :, D:D_EXT, :], in_=kx[:, :, 0:HALF, :])
-            kk = work.tile([P, N_BLOCKS, K_PASS], BF16, name="kk", align_bytes=64)
+            state[("kn_tok", g)] = kn_tok
+            state[("kx", g)] = kx
+
+        def back_b(g):
+            vT = state[("vT", g)]
+            kx = state[("kx", g)]
+            v_tok = ps_misc.tile([P, PACK, P], F32, name="v_tok", tag="misc")
+            for t in range(PACK):
+                nc.tensor.transpose(out=v_tok[:, t, :], in_=vT[:, P * t : P * t + P], identity=ident[:])
+            kk_v = work.tile([P, V_DIAGS + 1, K_PASS], BF16, name="kk_v", align_bytes=64)
             kx_flat = kx[:, :, 0:D, :].rearrange("p h d t -> p h (d t)")
             nc.scalar.activation(
-                out=kk[:, 0, :].rearrange("p (h n) -> p h n", h=H), in_=kx_flat, func=ACT.Square
+                out=kk_v[:, 0, :].rearrange("p (h n) -> p h n", h=H), in_=kx_flat, func=ACT.Square
             )
-            nc.scalar.copy(out=kk[:, N_DIAG, :].rearrange("p (h n) -> p h n", h=H), in_=kx_flat)
+            nc.scalar.copy(out=kk_v[:, V_DIAGS, :].rearrange("p (h n) -> p h n", h=H), in_=kx_flat)
             nc.scalar.copy(
                 out=knp[g % 4][:, :, 0:P].rearrange("p t (h d) -> p t h d", h=H),
                 in_=kx[:, :, 0:D, :].rearrange("p h d t -> p t h d"),
@@ -184,51 +220,63 @@ def tile_taylorsoftmaxattention_pa_t_kernel(tc, x, Wk, bk, Wv, bv, out_0, out_1,
             nc.scalar.copy(
                 out=vb[:].rearrange("p (f t) -> p f t", t=PACK), in_=v_tok[:].rearrange("p t f -> p f t")
             )
+            state[("kk_v", g)] = kk_v
+            state[("vb", g)] = vb
+
+        def quant_v(g):
             v_codes = keep.tile([P, P], U32, name="v_codes", align_bytes=64)
             v_scales = keep.tile([P, P], U8, name="v_scales", align_bytes=64)
-            nc.vector.quantize_mx(out=v_codes[:].bitcast(FP8X4), scales=v_scales[:], in_=vb[:])
-            state[("kn_tok", g)] = kn_tok
-            state[("kx", g)] = kx
-            state[("kk", g)] = kk
+            nc.vector.quantize_mx(out=v_codes[:].bitcast(FP8X4), scales=v_scales[:], in_=state[("vb", g)][:])
             state[("v", g)] = (v_codes, v_scales)
 
-        def products(g):
+        def mult(g):
             kn_tok = state[("kn_tok", g)]
             kx = state[("kx", g)]
-            kk = state[("kk", g)]
-            kk_codes = keep.tile([P, N_BLOCKS * P], U32, name="kk_codes", align_bytes=64)
-            kk_scales = keep.tile([P, N_BLOCKS * P], U8, name="kk_scales", align_bytes=64)
-
-            def quantise(lo, hi):
-                nc.vector.quantize_mx(
-                    out=kk_codes[:, P * lo : P * hi].bitcast(FP8X4),
-                    scales=kk_scales[:, P * lo : P * hi],
-                    in_=kk[:, lo:hi, :].rearrange("p a n -> p (a n)"),
-                )
-
-            for dd in range(HALF - GP_DIAGS + 1, HALF + 1):
+            kk_v = state[("kk_v", g)]
+            kk_g = const.tile([P, GP_DIAGS, K_PASS], BF16, name="kk_g", align_bytes=64)
+            for j in range(GP_DIAGS):
+                dd = V_DIAGS + j
                 nc.gpsimd.tensor_tensor(
-                    out=kk[:, dd, :].rearrange("p (h n) -> p h n", h=H),
+                    out=kk_g[:, j, :].rearrange("p (h n) -> p h n", h=H),
                     in0=kx[:, :, 0:D, :].rearrange("p h d t -> p h (d t)"),
                     in1=kx[:, :, dd : dd + D, :].rearrange("p h d t -> p h (d t)"),
                     op=ALU.mult,
                 )
-            for dd in range(1, HALF - GP_DIAGS + 1):
+            for dd in range(1, V_DIAGS):
                 nc.vector.tensor_tensor(
-                    out=kk[:, dd, :].rearrange("p (h d t) -> p h d t", h=H, t=PACK),
+                    out=kk_v[:, dd, :].rearrange("p (h d t) -> p h d t", h=H, t=PACK),
                     in0=kn_tok[:].rearrange("p t (h d) -> p h d t", h=H),
                     in1=kx[:, :, dd : dd + D, :],
                     op=ALU.mult,
                 )
-                if dd == 8:
-                    quantise(0, 8)
-            quantise(8, 16)
-            quantise(16, 18)
+            state[("kk_g", g)] = kk_g
+
+        def quant_kk(g):
+            kk_codes = keep.tile([P, N_BLOCKS * P], U32, name="kk_codes", align_bytes=64)
+            kk_scales = keep.tile([P, N_BLOCKS * P], U8, name="kk_scales", align_bytes=64)
+
+            def quantise_blocks(src, first_src, first_code, count):
+                done = 0
+                for size in (8, 4, 2, 1):
+                    if count - done >= size:
+                        lo = first_code + done
+                        nc.vector.quantize_mx(
+                            out=kk_codes[:, P * lo : P * (lo + size)].bitcast(FP8X4),
+                            scales=kk_scales[:, P * lo : P * (lo + size)],
+                            in_=src[:, first_src + done : first_src + done + size, :].rearrange("p a n -> p (a n)"),
+                        )
+                        done += size
+
+            quantise_blocks(state[("kk_v", g)], 0, 0, V_DIAGS)
+            quantise_blocks(state[("kk_v", g)], V_DIAGS, N_DIAG, 1)
+            quantise_blocks(state[("kk_g", g)], 0, V_DIAGS, GP_DIAGS)
             state[("kkq", g)] = (kk_codes, kk_scales)
 
-        def moments(b):
-            u_sb = work.tile([P, N_BLOCKS, D], F32, name="u_sb", align_bytes=64)
-            for w in range(5):
+        def stage2_windows(b, first, last):
+            if first == 0:
+                state[("u_sb", b)] = work.tile([P, N_BLOCKS, D], F32, name="u_sb", align_bytes=64)
+            u_sb = state[("u_sb", b)]
+            for w in range(first, last):
                 n = min(4, N_BLOCKS - 4 * w) * P
                 acc2 = ps_misc.tile([P, K_PASS], F32, name="acc2", tag="misc")
                 for j in range(2):
@@ -250,6 +298,9 @@ def tile_taylorsoftmaxattention_pa_t_kernel(tc, x, Wk, bk, Wv, bv, out_0, out_1,
                         out=u_sb[rows, 4 * w : 4 * w + n // P, :],
                         in_=acc2[rows, 0:n].rearrange("p (a k i) -> p a k i", k=H, i=D)[:, :, h, :],
                     )
+
+        def unskew(b):
+            u_sb = state[("u_sb", b)]
             a_flat = a_mat[b % 2]
             a_skew = a_flat[:].rearrange("p (i q) -> p i q", q=A_PITCH + 1)
             a_rows = a_flat[:, 0 : D * A_PITCH].rearrange("p (r c) -> p r c", c=A_PITCH)
@@ -258,19 +309,9 @@ def tile_taylorsoftmaxattention_pa_t_kernel(tc, x, Wk, bk, Wv, bv, out_0, out_1,
             nc.scalar.copy(out=a_skew[:, :, 1:HALF], in_=u_id[:, :, 1:HALF])
             nc.scalar.copy(out=a_skew[:, 0:HALF, HALF : HALF + 1], in_=u_id[:, 0:HALF, HALF : HALF + 1])
             nc.scalar.copy(out=a_rows[:, HALF:D, 0:HALF], in_=a_rows[:, HALF:D, D:D_EXT])
+            state[("a_rows", b)] = a_rows
 
-            sym = work.tile([P, D * D], F32, name="sym", align_bytes=64)
-            nc.vector.tensor_tensor(
-                out=sym[:].rearrange("p (r c) -> p r c", c=D),
-                in0=a_rows[:, :, 0:D],
-                in1=a_rows[:, :, 0:D].rearrange("p r c -> p c r"),
-                op=ALU.add,
-            )
-            turned = work.tile([P, D * D], F32, name="turned", align_bytes=64)
-            nc.vector.transpose(out=turned[:], in_=sym[:])
-            kv_turned = work.tile([P, D], F32, name="kv_turned", align_bytes=64)
-            nc.vector.transpose(out=kv_turned[:], in_=u_sb[:, N_DIAG, :])
-
+        def plain_sums(b):
             gram = ps_misc.tile([P, P + 1], F32, name="gram", tag="misc")
             for j in range(2):
                 for t in range(PACK):
@@ -290,6 +331,31 @@ def tile_taylorsoftmaxattention_pa_t_kernel(tc, x, Wk, bk, Wv, bv, out_0, out_1,
                     out=fin[rows, :, 0:1], in_=gram[rows, D * h : D * h + D].unsqueeze(2), mul=1.0 / N_TOK
                 )
             nc.scalar.mul(out=kvf[:, 0:1], in_=gram[:, P : P + 1], mul=1.0 / N_TOK)
+            state[("fin", b)] = (fin, kvf)
+
+        def symmetrise(b):
+            a_rows = state[("a_rows", b)]
+            sym = work.tile([P, D * D], F32, name="sym", align_bytes=64)
+            nc.vector.tensor_tensor(
+                out=sym[:].rearrange("p (r c) -> p r c", c=D),
+                in0=a_rows[:, :, 0:D],
+                in1=a_rows[:, :, 0:D].rearrange("p r c -> p c r"),
+                op=ALU.add,
+            )
+            state[("sym", b)] = sym
+
+        def turn(b):
+            sym = state[("sym", b)]
+            u_sb = state[("u_sb", b)]
+            turned = work.tile([P, D * D], F32, name="turned", align_bytes=64)
+            nc.vector.transpose(out=turned[:], in_=sym[:])
+            kv_turned = work.tile([P, D], F32, name="kv_turned", align_bytes=64)
+            nc.vector.transpose(out=kv_turned[:], in_=u_sb[:, N_DIAG, :])
+            state[("turned", b)] = (turned, kv_turned)
+
+        def store(b):
+            fin, kvf = state[("fin", b)]
+            turned, kv_turned = state[("turned", b)]
             nc.scalar.copy(out=fin[:, :, 1 : D + 1], in_=turned[:].rearrange("p (j e) -> p j e", e=D))
             nc.scalar.copy(out=kvf[:, 1 : D + 1], in_=kv_turned[:])
             nc.scalar.dma_start(
@@ -297,23 +363,53 @@ def tile_taylorsoftmaxattention_pa_t_kernel(tc, x, Wk, bk, Wv, bv, out_0, out_1,
             )
             nc.scalar.dma_start(out=out_1[b].rearrange("h d e -> (h d) e"), in_=kvf[:])
 
-        front(0)
-        for g in range(GROUPS):
-            if g + 1 < GROUPS:
-                front(g + 1)
-            products(g)
-            if g % 2 == 1:
-                moments(g // 2)
+        def value_sums():
+            vs_pairs = vs_cols[:].rearrange("p (b j) -> p b j", j=2)
+            nc.vector.tensor_tensor(out=vs_pad[:, 0:B], in0=vs_pairs[:, :, 0], in1=vs_pairs[:, :, 1], op=ALU.add)
+            vs_ps = ps_misc.tile([P, P], F32, name="vs_ps", tag="misc")
+            nc.tensor.transpose(out=vs_ps[:], in_=vs_pad[:], identity=ident[:])
+            nc.vector.tensor_copy(out=vs_fin[:, :, 1 : D + 1], in_=vs_ps[:].rearrange("p (h e) -> p h e", h=H))
+            nc.sync.dma_start(
+                out=out_2.rearrange("b h o e -> b (h o e)"), in_=vs_fin[0:B, :, :].rearrange("p h e -> p (h e)")
+            )
 
-        vs_pad = const.tile([P, P], F32, name="vs_pad")
-        nc.vector.memset(vs_pad[:], 0.0)
-        vs_pairs = vs_cols[:].rearrange("p (b j) -> p b j", j=2)
-        nc.vector.tensor_tensor(out=vs_pad[:, 0:B], in0=vs_pairs[:, :, 0], in1=vs_pairs[:, :, 1], op=ALU.add)
-        vs_ps = ps_misc.tile([P, P], F32, name="vs_ps", tag="misc")
-        nc.tensor.transpose(out=vs_ps[:], in_=vs_pad[:], identity=ident[:])
-        vs_fin = const.tile([P, H, D + 1], F32, name="vs_fin")
-        nc.vector.memset(vs_fin[:], 1.0)
-        nc.vector.tensor_copy(out=vs_fin[:, :, 1 : D + 1], in_=vs_ps[:].rearrange("p (h e) -> p h e", h=H))
-        nc.sync.dma_start(
-            out=out_2.rearrange("b h o e -> b (h o e)"), in_=vs_fin[0:B, :, :].rearrange("p h e -> p (h e)")
-        )
+        def on(g):
+            return 0 <= g < GROUPS
+
+        n_windows = (N_BLOCKS + 3) // 4
+        for s in range(-3, GROUPS + 2):
+            closing = s >= 2 and s % 2 == 0
+            finishing = s >= 3 and s % 2 == 1
+            if on(s):
+                mult(s)
+            if finishing:
+                symmetrise((s - 3) // 2)
+            if on(s + 1):
+                norm_k(s + 1)
+                back_a(s + 1)
+            if on(s + 2):
+                quant_x(s + 2)
+                project_a(s + 2)
+            if on(s + 1):
+                back_b(s + 1)
+            if on(s + 2):
+                project_b(s + 2)
+            if closing:
+                stage2_windows(s // 2 - 1, WINDOWS_EARLY, n_windows)
+                unskew(s // 2 - 1)
+                plain_sums(s // 2 - 1)
+            if on(s):
+                quant_v(s)
+                quant_kk(s)
+            if finishing:
+                turn((s - 3) // 2)
+            if on(s + 3):
+                turn_x(s + 3)
+            if on(s + 6):
+                load_x(s + 6)
+            if finishing:
+                store((s - 3) // 2)
+            if s == GROUPS - 2:
+                value_sums()
+            if on(s) and s % 2 == 1:
+                stage2_windows(s // 2, 0, WINDOWS_EARLY)

@@ -27,7 +27,7 @@ N_BLOCKS = N_DIAG + 1
 A_PITCH = D_EXT
 EPS = 1e-12
 SCALE = 32.0 ** 0.25
-GP_DIAGS = 5
+GP_DIAGS = 4
 V_DIAGS = N_DIAG - GP_DIAGS
 WINDOWS_EARLY = 3
 
@@ -106,6 +106,8 @@ def tile_taylorsoftmaxattention_pa_t_kernel(tc, x, Wk, bk, Wv, bv, out_0, out_1,
         a_mat = [const.tile([P, D * (A_PITCH + 1)], F32, name="a_mat%d" % i) for i in range(2)]
         for t in a_mat:
             nc.vector.memset(t[:], 0.0)
+        kk_g = const.tile([P, GP_DIAGS, K_PASS], BF16, name="kk_g", align_bytes=64)
+        nc.vector.memset(kk_g[:, GP_DIAGS - 1, :], 0.0)
         vs_cols = const.tile([P, GROUPS], F32, name="vs_cols")
         vs_pad = const.tile([P, P], F32, name="vs_pad")
         nc.vector.memset(vs_pad[:], 0.0)
@@ -233,13 +235,13 @@ def tile_taylorsoftmaxattention_pa_t_kernel(tc, x, Wk, bk, Wv, bv, out_0, out_1,
             kn_tok = state[("kn_tok", g)]
             kx = state[("kx", g)]
             kk_v = state[("kk_v", g)]
-            kk_g = const.tile([P, GP_DIAGS, K_PASS], BF16, name="kk_g", align_bytes=64)
             for j in range(GP_DIAGS):
                 dd = V_DIAGS + j
+                n_i = HALF if dd == HALF else D
                 nc.gpsimd.tensor_tensor(
-                    out=kk_g[:, j, :].rearrange("p (h n) -> p h n", h=H),
-                    in0=kx[:, :, 0:D, :].rearrange("p h d t -> p h (d t)"),
-                    in1=kx[:, :, dd : dd + D, :].rearrange("p h d t -> p h (d t)"),
+                    out=kk_g[:, j, :].rearrange("p (h n) -> p h n", h=H)[:, :, 0 : n_i * PACK],
+                    in0=kx[:, :, 0:n_i, :].rearrange("p h d t -> p h (d t)"),
+                    in1=kx[:, :, dd : dd + n_i, :].rearrange("p h d t -> p h (d t)"),
                     op=ALU.mult,
                 )
             for dd in range(1, V_DIAGS):
@@ -249,7 +251,6 @@ def tile_taylorsoftmaxattention_pa_t_kernel(tc, x, Wk, bk, Wv, bv, out_0, out_1,
                     in1=kx[:, :, dd : dd + D, :],
                     op=ALU.mult,
                 )
-            state[("kk_g", g)] = kk_g
 
         def quant_kk(g):
             kk_codes = keep.tile([P, N_BLOCKS * P], U32, name="kk_codes", align_bytes=64)
@@ -269,7 +270,7 @@ def tile_taylorsoftmaxattention_pa_t_kernel(tc, x, Wk, bk, Wv, bv, out_0, out_1,
 
             quantise_blocks(state[("kk_v", g)], 0, 0, V_DIAGS)
             quantise_blocks(state[("kk_v", g)], V_DIAGS, N_DIAG, 1)
-            quantise_blocks(state[("kk_g", g)], 0, V_DIAGS, GP_DIAGS)
+            quantise_blocks(kk_g, 0, V_DIAGS, GP_DIAGS)
             state[("kkq", g)] = (kk_codes, kk_scales)
 
         def stage2_windows(b, first, last):

@@ -28,7 +28,7 @@ A_PITCH = D_EXT
 EPS = 1e-12
 SCALE = 32.0 ** 0.25
 GP_DIAGS = 4
-V_DIAGS = N_DIAG - GP_DIAGS
+V_DIAGS = HALF - GP_DIAGS
 WINDOWS_EARLY = 3
 
 FLOPS = 2 * B * N_TOK * C * 2 * H * D + 2 * B * H * N_TOK * (D * D + D) * D
@@ -41,9 +41,9 @@ def tile_taylorsoftmaxattention_pa_t_kernel(tc, x, Wk, bk, Wv, bv, out_0, out_1,
         xpool = ctx.enter_context(tc.tile_pool(name="xpool", bufs=3))
         work = ctx.enter_context(tc.tile_pool(name="work", bufs=2))
         keep = ctx.enter_context(tc.tile_pool(name="keep", bufs=4))
-        ps_xt = ctx.enter_context(tc.psum_pool(name="ps_xt", bufs=2))
+        ps_xt = ctx.enter_context(tc.psum_pool(name="ps_xt", bufs=3))
         ps_s1 = ctx.enter_context(tc.psum_pool(name="ps_s1", bufs=2))
-        ps_kn = ctx.enter_context(tc.psum_pool(name="ps_kn", bufs=2))
+        ps_kn = ctx.enter_context(tc.psum_pool(name="ps_kn", bufs=1))
         ps_misc = ctx.enter_context(tc.psum_pool(name="ps_misc", bufs=2))
 
         state = {}
@@ -106,8 +106,8 @@ def tile_taylorsoftmaxattention_pa_t_kernel(tc, x, Wk, bk, Wv, bv, out_0, out_1,
         a_mat = [const.tile([P, D * (A_PITCH + 1)], F32, name="a_mat%d" % i) for i in range(2)]
         for t in a_mat:
             nc.vector.memset(t[:], 0.0)
-        kk_g = const.tile([P, GP_DIAGS, K_PASS], BF16, name="kk_g", align_bytes=64)
-        nc.vector.memset(kk_g[:, GP_DIAGS - 1, :], 0.0)
+        kk_g = const.tile([P, GP_DIAGS + 2, K_PASS], BF16, name="kk_g", align_bytes=64)
+        nc.vector.memset(kk_g[:, GP_DIAGS, :], 0.0)
         vs_cols = const.tile([P, GROUPS], F32, name="vs_cols")
         vs_pad = const.tile([P, P], F32, name="vs_pad")
         nc.vector.memset(vs_pad[:], 0.0)
@@ -208,12 +208,6 @@ def tile_taylorsoftmaxattention_pa_t_kernel(tc, x, Wk, bk, Wv, bv, out_0, out_1,
             v_tok = ps_misc.tile([P, PACK, P], F32, name="v_tok", tag="misc")
             for t in range(PACK):
                 nc.tensor.transpose(out=v_tok[:, t, :], in_=vT[:, P * t : P * t + P], identity=ident[:])
-            kk_v = work.tile([P, V_DIAGS + 1, K_PASS], BF16, name="kk_v", align_bytes=64)
-            kx_flat = kx[:, :, 0:D, :].rearrange("p h d t -> p h (d t)")
-            nc.scalar.activation(
-                out=kk_v[:, 0, :].rearrange("p (h n) -> p h n", h=H), in_=kx_flat, func=ACT.Square
-            )
-            nc.scalar.copy(out=kk_v[:, V_DIAGS, :].rearrange("p (h n) -> p h n", h=H), in_=kx_flat)
             nc.scalar.copy(
                 out=knp[g % 4][:, :, 0:P].rearrange("p t (h d) -> p t h d", h=H),
                 in_=kx[:, :, 0:D, :].rearrange("p h d t -> p t h d"),
@@ -222,7 +216,6 @@ def tile_taylorsoftmaxattention_pa_t_kernel(tc, x, Wk, bk, Wv, bv, out_0, out_1,
             nc.scalar.copy(
                 out=vb[:].rearrange("p (f t) -> p f t", t=PACK), in_=v_tok[:].rearrange("p t f -> p f t")
             )
-            state[("kk_v", g)] = kk_v
             state[("vb", g)] = vb
 
         def quant_v(g):
@@ -234,8 +227,9 @@ def tile_taylorsoftmaxattention_pa_t_kernel(tc, x, Wk, bk, Wv, bv, out_0, out_1,
         def mult(g):
             kn_tok = state[("kn_tok", g)]
             kx = state[("kx", g)]
-            kk_v = state[("kk_v", g)]
-            for j in range(GP_DIAGS):
+            kk_v = work.tile([P, V_DIAGS, K_PASS], BF16, name="kk_v", align_bytes=64)
+            kx_flat = kx[:, :, 0:D, :].rearrange("p h d t -> p h (d t)")
+            for j in range(1, GP_DIAGS + 1):
                 dd = V_DIAGS + j
                 n_i = HALF if dd == HALF else D
                 nc.gpsimd.tensor_tensor(
@@ -244,13 +238,25 @@ def tile_taylorsoftmaxattention_pa_t_kernel(tc, x, Wk, bk, Wv, bv, out_0, out_1,
                     in1=kx[:, :, dd : dd + n_i, :].rearrange("p h d t -> p h (d t)"),
                     op=ALU.mult,
                 )
-            for dd in range(1, V_DIAGS):
+            nc.gpsimd.tensor_scalar(
+                out=kk_g[:, GP_DIAGS + 1, :].rearrange("p (h n) -> p h n", h=H),
+                in0=kx_flat,
+                scalar1=1.0,
+                scalar2=0.0,
+                op0=ALU.mult,
+                op1=ALU.add,
+            )
+            nc.gpsimd.tensor_tensor(
+                out=kk_g[:, 0, :].rearrange("p (h n) -> p h n", h=H), in0=kx_flat, in1=kx_flat, op=ALU.mult
+            )
+            for dd in range(1, V_DIAGS + 1):
                 nc.vector.tensor_tensor(
-                    out=kk_v[:, dd, :].rearrange("p (h d t) -> p h d t", h=H, t=PACK),
+                    out=kk_v[:, dd - 1, :].rearrange("p (h d t) -> p h d t", h=H, t=PACK),
                     in0=kn_tok[:].rearrange("p t (h d) -> p h d t", h=H),
                     in1=kx[:, :, dd : dd + D, :],
                     op=ALU.mult,
                 )
+            state[("kk_v", g)] = kk_v
 
         def quant_kk(g):
             kk_codes = keep.tile([P, N_BLOCKS * P], U32, name="kk_codes", align_bytes=64)
@@ -268,9 +274,9 @@ def tile_taylorsoftmaxattention_pa_t_kernel(tc, x, Wk, bk, Wv, bv, out_0, out_1,
                         )
                         done += size
 
-            quantise_blocks(state[("kk_v", g)], 0, 0, V_DIAGS)
-            quantise_blocks(state[("kk_v", g)], V_DIAGS, N_DIAG, 1)
-            quantise_blocks(kk_g, 0, V_DIAGS, GP_DIAGS)
+            quantise_blocks(state[("kk_v", g)], 0, 1, V_DIAGS)
+            quantise_blocks(kk_g, 1, V_DIAGS + 1, GP_DIAGS + 1)
+            quantise_blocks(kk_g, 0, 0, 1)
             state[("kkq", g)] = (kk_codes, kk_scales)
 
         def stage2_windows(b, first, last):

@@ -7,6 +7,7 @@ F32 = mybir.dt.float32
 BF16 = mybir.dt.bfloat16
 U32 = mybir.dt.uint32
 U8 = mybir.dt.uint8
+I32 = mybir.dt.int32
 FP8X4 = mybir.dt.float8_e4m3fn_x4
 ACT = mybir.ActivationFunctionType
 ALU = mybir.AluOpType
@@ -27,9 +28,12 @@ N_BLOCKS = N_DIAG + 1
 A_PITCH = D_EXT
 EPS = 1e-12
 SCALE = 32.0 ** 0.25
-GP_DIAGS = 4
+GP_DIAGS = 5
 V_DIAGS = HALF - GP_DIAGS
-WINDOWS_EARLY = 3
+BLOCK = D * PACK
+HEAD_WORDS = N_BLOCKS * D
+KK_WORDS = H * HEAD_WORDS
+TAIL = 2 * D
 
 FLOPS = 2 * B * N_TOK * C * 2 * H * D + 2 * B * H * N_TOK * (D * D + D) * D
 
@@ -106,8 +110,16 @@ def tile_taylorsoftmaxattention_pa_t_kernel(tc, x, Wk, bk, Wv, bv, out_0, out_1,
         a_mat = [const.tile([P, D * (A_PITCH + 1)], F32, name="a_mat%d" % i) for i in range(2)]
         for t in a_mat:
             nc.vector.memset(t[:], 0.0)
-        kk_g = const.tile([P, GP_DIAGS + 2, K_PASS], BF16, name="kk_g", align_bytes=64)
-        nc.vector.memset(kk_g[:, GP_DIAGS, :], 0.0)
+        kk = const.tile([P, H * N_BLOCKS * BLOCK], BF16, name="kk", align_bytes=64)
+        kk_blocks = kk[:].rearrange("p (h a n) -> p h a n", h=H, a=N_BLOCKS)
+        nc.vector.memset(kk_blocks[:, :, HALF - 1, :], 0.0)
+        kk_codes = [const.tile([P, KK_WORDS + TAIL], U32, name="kk_codes%d" % i, align_bytes=64) for i in range(4)]
+        kk_scales = [const.tile([P, KK_WORDS + TAIL], U8, name="kk_scales%d" % i, align_bytes=64) for i in range(4)]
+        for t in kk_codes + kk_scales:
+            nc.vector.memset(t[:, KK_WORDS : KK_WORDS + TAIL], 0)
+        v_masked = [const.tile([P, H * (P + D)], U32, name="v_masked%d" % i, align_bytes=64) for i in range(4)]
+        for t in v_masked:
+            nc.vector.memset(t[:], 0)
         vs_cols = const.tile([P, GROUPS], F32, name="vs_cols")
         vs_pad = const.tile([P, P], F32, name="vs_pad")
         nc.vector.memset(vs_pad[:], 0.0)
@@ -209,8 +221,8 @@ def tile_taylorsoftmaxattention_pa_t_kernel(tc, x, Wk, bk, Wv, bv, out_0, out_1,
             for t in range(PACK):
                 nc.tensor.transpose(out=v_tok[:, t, :], in_=vT[:, P * t : P * t + P], identity=ident[:])
             nc.scalar.copy(
-                out=knp[g % 4][:, :, 0:P].rearrange("p t (h d) -> p t h d", h=H),
-                in_=kx[:, :, 0:D, :].rearrange("p h d t -> p t h d"),
+                out=knp[g % 4][:, :, 0:P].rearrange("p t (h d) -> p h d t", h=H),
+                in_=kx[:, :, 0:D, :],
             )
             vb = work.tile([P, K_PASS], BF16, name="vb", align_bytes=64)
             nc.scalar.copy(
@@ -224,99 +236,79 @@ def tile_taylorsoftmaxattention_pa_t_kernel(tc, x, Wk, bk, Wv, bv, out_0, out_1,
             nc.vector.quantize_mx(out=v_codes[:].bitcast(FP8X4), scales=v_scales[:], in_=state[("vb", g)][:])
             state[("v", g)] = (v_codes, v_scales)
 
+        def mask_v(g):
+            v_codes, v_scales = state[("v", g)]
+            nc.vector.tensor_copy(
+                out=v_masked[g % 4][:].bitcast(I32).rearrange("p (h q) -> p h q", h=H)[:, :, 0:D],
+                in_=v_codes[:].bitcast(I32).rearrange("p (h d) -> p h d", h=H),
+            )
+
         def mult(g):
             kn_tok = state[("kn_tok", g)]
             kx = state[("kx", g)]
-            kk_v = work.tile([P, V_DIAGS, K_PASS], BF16, name="kk_v", align_bytes=64)
+            kn_hdt = kn_tok[:].rearrange("p t (h d) -> p h d t", h=H)
             kx_flat = kx[:, :, 0:D, :].rearrange("p h d t -> p h (d t)")
-            for j in range(1, GP_DIAGS + 1):
-                dd = V_DIAGS + j
+            nc.scalar.activation(out=kk_blocks[:, :, HALF, :], in_=kx_flat, func=ACT.Square)
+            nc.scalar.copy(out=kk_blocks[:, :, HALF + 1, :], in_=kx_flat)
+            for dd in range(V_DIAGS + 1, HALF + 1):
                 n_i = HALF if dd == HALF else D
                 nc.gpsimd.tensor_tensor(
-                    out=kk_g[:, j, :].rearrange("p (h n) -> p h n", h=H)[:, :, 0 : n_i * PACK],
+                    out=kk_blocks[:, :, dd - 1, 0 : n_i * PACK],
                     in0=kx[:, :, 0:n_i, :].rearrange("p h d t -> p h (d t)"),
                     in1=kx[:, :, dd : dd + n_i, :].rearrange("p h d t -> p h (d t)"),
                     op=ALU.mult,
                 )
-            nc.gpsimd.tensor_scalar(
-                out=kk_g[:, GP_DIAGS + 1, :].rearrange("p (h n) -> p h n", h=H),
-                in0=kx_flat,
-                scalar1=1.0,
-                scalar2=0.0,
-                op0=ALU.mult,
-                op1=ALU.add,
-            )
-            nc.gpsimd.tensor_tensor(
-                out=kk_g[:, 0, :].rearrange("p (h n) -> p h n", h=H), in0=kx_flat, in1=kx_flat, op=ALU.mult
-            )
             for dd in range(1, V_DIAGS + 1):
                 nc.vector.tensor_tensor(
-                    out=kk_v[:, dd - 1, :].rearrange("p (h d t) -> p h d t", h=H, t=PACK),
-                    in0=kn_tok[:].rearrange("p t (h d) -> p h d t", h=H),
+                    out=kk_blocks[:, :, dd - 1, :].rearrange("p h (d t) -> p h d t", t=PACK),
+                    in0=kn_hdt,
                     in1=kx[:, :, dd : dd + D, :],
                     op=ALU.mult,
                 )
-            state[("kk_v", g)] = kk_v
 
         def quant_kk(g):
-            kk_codes = keep.tile([P, N_BLOCKS * P], U32, name="kk_codes", align_bytes=64)
-            kk_scales = keep.tile([P, N_BLOCKS * P], U8, name="kk_scales", align_bytes=64)
+            done = 0
+            for size in (4096, 4096, 1024):
+                words = slice(done // PACK, (done + size) // PACK)
+                nc.vector.quantize_mx(
+                    out=kk_codes[g % 4][:, words].bitcast(FP8X4),
+                    scales=kk_scales[g % 4][:, words],
+                    in_=kk[:, done : done + size],
+                )
+                done += size
 
-            def quantise_blocks(src, first_src, first_code, count):
-                done = 0
-                for size in (8, 4, 2, 1):
-                    if count - done >= size:
-                        lo = first_code + done
-                        nc.vector.quantize_mx(
-                            out=kk_codes[:, P * lo : P * (lo + size)].bitcast(FP8X4),
-                            scales=kk_scales[:, P * lo : P * (lo + size)],
-                            in_=src[:, first_src + done : first_src + done + size, :].rearrange("p a n -> p (a n)"),
-                        )
-                        done += size
-
-            quantise_blocks(state[("kk_v", g)], 0, 1, V_DIAGS)
-            quantise_blocks(kk_g, 1, V_DIAGS + 1, GP_DIAGS + 1)
-            quantise_blocks(kk_g, 0, 0, 1)
-            state[("kkq", g)] = (kk_codes, kk_scales)
-
-        def stage2_windows(b, first, last):
-            if first == 0:
-                state[("u_sb", b)] = work.tile([P, N_BLOCKS, D], F32, name="u_sb", align_bytes=64)
-            u_sb = state[("u_sb", b)]
-            for w in range(first, last):
-                n = min(4, N_BLOCKS - 4 * w) * P
-                acc2 = ps_misc.tile([P, K_PASS], F32, name="acc2", tag="misc")
-                for j in range(2):
-                    v_codes, v_scales = state[("v", 2 * b + j)]
-                    kk_codes, kk_scales = state[("kkq", 2 * b + j)]
-                    cols = slice(K_PASS * w, K_PASS * w + n)
-                    nc.tensor.matmul_mx(
-                        out=acc2[:, 0:n],
-                        lhsT=v_codes[:].bitcast(FP8X4),
-                        lhsT_scale=v_scales[:],
-                        rhs=kk_codes[:, cols].bitcast(FP8X4),
-                        rhs_scale=kk_scales[:, cols],
-                        start=(j == 0),
-                        stop=(j == 1),
-                    )
+        def stage2(b):
+            u1 = ps_misc.tile([P, K_PASS], F32, name="u1", tag="misc")
+            u2 = ps_misc.tile([P, P], F32, name="u2", tag="misc")
+            for j in range(2):
+                g = 2 * b + j
+                v_scales = state[("v", g)][1]
                 for h in range(H):
-                    rows = slice(D * h, D * h + D)
-                    nc.scalar.copy(
-                        out=u_sb[rows, 4 * w : 4 * w + n // P, :],
-                        in_=acc2[rows, 0:n].rearrange("p (a k i) -> p a k i", k=H, i=D)[:, :, h, :],
-                    )
+                    for out, first, n in ((u1, 0, K_PASS), (u2, K_PASS, P)):
+                        cols = slice(HEAD_WORDS * h + first, HEAD_WORDS * h + first + n)
+                        nc.tensor.matmul_mx(
+                            out=out[:],
+                            lhsT=v_masked[g % 4][:, P * h : P * h + P].bitcast(FP8X4),
+                            lhsT_scale=v_scales[:],
+                            rhs=kk_codes[g % 4][:, cols].bitcast(FP8X4),
+                            rhs_scale=kk_scales[g % 4][:, cols],
+                            start=(j == 0 and h == 0),
+                            stop=(j == 1 and h == H - 1),
+                        )
+            state[("u", b)] = (u1, u2)
 
         def unskew(b):
-            u_sb = state[("u_sb", b)]
+            u1, u2 = state[("u", b)]
             a_flat = a_mat[b % 2]
             a_skew = a_flat[:].rearrange("p (i q) -> p i q", q=A_PITCH + 1)
             a_rows = a_flat[:, 0 : D * A_PITCH].rearrange("p (r c) -> p r c", c=A_PITCH)
-            u_id = u_sb[:].rearrange("p a i -> p i a")
-            nc.scalar.mul(out=a_skew[:, :, 0:1], in_=u_id[:, :, 0:1], mul=0.5)
-            nc.scalar.copy(out=a_skew[:, :, 1:HALF], in_=u_id[:, :, 1:HALF])
-            nc.scalar.copy(out=a_skew[:, 0:HALF, HALF : HALF + 1], in_=u_id[:, 0:HALF, HALF : HALF + 1])
+            nc.scalar.copy(out=a_skew[:, :, 1 : HALF + 1], in_=u1[:].rearrange("p (a i) -> p i a", i=D))
+            nc.scalar.mul(out=a_skew[:, :, 0:1], in_=u2[:, 0:D].unsqueeze(2), mul=0.5)
+            kv_sb = work.tile([P, D], F32, name="kv_sb", align_bytes=64)
+            nc.scalar.copy(out=kv_sb[:], in_=u2[:, D : 2 * D])
             nc.scalar.copy(out=a_rows[:, HALF:D, 0:HALF], in_=a_rows[:, HALF:D, D:D_EXT])
             state[("a_rows", b)] = a_rows
+            state[("kv_sb", b)] = kv_sb
 
         def plain_sums(b):
             gram = ps_misc.tile([P, P + 1], F32, name="gram", tag="misc")
@@ -344,20 +336,19 @@ def tile_taylorsoftmaxattention_pa_t_kernel(tc, x, Wk, bk, Wv, bv, out_0, out_1,
             a_rows = state[("a_rows", b)]
             sym = work.tile([P, D * D], F32, name="sym", align_bytes=64)
             nc.vector.tensor_tensor(
-                out=sym[:].rearrange("p (r c) -> p r c", c=D),
-                in0=a_rows[:, :, 0:D],
-                in1=a_rows[:, :, 0:D].rearrange("p r c -> p c r"),
+                out=sym[:].rearrange("p (r c v) -> p c r v", r=D, v=4),
+                in0=a_rows[:, :, 0:D].rearrange("p r (c v) -> p c r v", v=4),
+                in1=a_rows[:, :, 0:D].rearrange("p (c v) r -> p c r v", v=4),
                 op=ALU.add,
             )
             state[("sym", b)] = sym
 
         def turn(b):
             sym = state[("sym", b)]
-            u_sb = state[("u_sb", b)]
             turned = work.tile([P, D * D], F32, name="turned", align_bytes=64)
             nc.vector.transpose(out=turned[:], in_=sym[:])
             kv_turned = work.tile([P, D], F32, name="kv_turned", align_bytes=64)
-            nc.vector.transpose(out=kv_turned[:], in_=u_sb[:, N_DIAG, :])
+            nc.vector.transpose(out=kv_turned[:], in_=state[("kv_sb", b)][:])
             state[("turned", b)] = (turned, kv_turned)
 
         def store(b):
@@ -383,7 +374,6 @@ def tile_taylorsoftmaxattention_pa_t_kernel(tc, x, Wk, bk, Wv, bv, out_0, out_1,
         def on(g):
             return 0 <= g < GROUPS
 
-        n_windows = (N_BLOCKS + 3) // 4
         for s in range(-3, GROUPS + 2):
             closing = s >= 2 and s % 2 == 0
             finishing = s >= 3 and s % 2 == 1
@@ -402,12 +392,13 @@ def tile_taylorsoftmaxattention_pa_t_kernel(tc, x, Wk, bk, Wv, bv, out_0, out_1,
             if on(s + 2):
                 project_b(s + 2)
             if closing:
-                stage2_windows(s // 2 - 1, WINDOWS_EARLY, n_windows)
+                stage2(s // 2 - 1)
                 unskew(s // 2 - 1)
                 plain_sums(s // 2 - 1)
             if on(s):
                 quant_v(s)
                 quant_kk(s)
+                mask_v(s)
             if finishing:
                 turn((s - 3) // 2)
             if on(s + 3):
@@ -418,5 +409,3 @@ def tile_taylorsoftmaxattention_pa_t_kernel(tc, x, Wk, bk, Wv, bv, out_0, out_1,
                 store((s - 3) // 2)
             if s == GROUPS - 2:
                 value_sums()
-            if on(s) and s % 2 == 1:
-                stage2_windows(s // 2, 0, WINDOWS_EARLY)

@@ -24,6 +24,8 @@ GROUPS = B * N_TOK // K_PASS
 HALF = D // 2
 N_DIAG = HALF + 1
 D_EXT = D + HALF
+K_EXT = 2 * D + HALF
+PAIR = D + 1
 N_BLOCKS = N_DIAG + 1
 A_PITCH = D_EXT
 EPS = 1e-12
@@ -208,9 +210,12 @@ def tile_taylorsoftmaxattention_pa_t_kernel(tc, x, Wk, bk, Wv, bv, out_0, out_1,
             kn_tok = ps_kn.tile([P, PACK, P], F32, name="kn_tok", tag="kn")
             for t in range(PACK):
                 nc.tensor.transpose(out=kn_tok[:, t, :], in_=knT[:, P * t : P * t + P], identity=ident[:])
-            kx = work.tile([P, H, D_EXT, PACK], F32, name="kx")
-            nc.scalar.copy(out=kx[:, :, 0:D, :], in_=kn_tok[:].rearrange("p t (h d) -> p h d t", h=H))
-            nc.scalar.copy(out=kx[:, :, D:D_EXT, :], in_=kx[:, :, 0:HALF, :])
+            kx = work.tile([P, H, K_EXT, PACK], F32, name="kx")
+            nc.scalar.copy(
+                out=kx[:, :, 0 : 2 * D, :].rearrange("p h (r d) t -> p r h d t", r=2),
+                in_=kn_tok[:].rearrange("p t (h d) -> p h d t", h=H).unsqueeze(1).to_broadcast([P, 2, H, D, PACK]),
+            )
+            nc.scalar.copy(out=kx[:, :, 2 * D : K_EXT, :], in_=kx[:, :, 0:HALF, :])
             state[("kn_tok", g)] = kn_tok
             state[("kx", g)] = kx
 
@@ -250,19 +255,25 @@ def tile_taylorsoftmaxattention_pa_t_kernel(tc, x, Wk, bk, Wv, bv, out_0, out_1,
             kx_flat = kx[:, :, 0:D, :].rearrange("p h d t -> p h (d t)")
             nc.scalar.activation(out=kk_blocks[:, :, HALF, :], in_=kx_flat, func=ACT.Square)
             nc.scalar.copy(out=kk_blocks[:, :, HALF + 1, :], in_=kx_flat)
-            for dd in range(V_DIAGS + 1, HALF + 1):
-                n_i = HALF if dd == HALF else D
+            for dd in range(V_DIAGS + 1, HALF, 2):
                 nc.gpsimd.tensor_tensor(
-                    out=kk_blocks[:, :, dd - 1, 0 : n_i * PACK],
-                    in0=kx[:, :, 0:n_i, :].rearrange("p h d t -> p h (d t)"),
-                    in1=kx[:, :, dd : dd + n_i, :].rearrange("p h d t -> p h (d t)"),
+                    out=kk_blocks[:, :, dd - 1 : dd + 1, :].rearrange("p h c n -> p c h n"),
+                    in0=kx_flat.unsqueeze(1).to_broadcast([P, 2, H, BLOCK]),
+                    in1=kx[:, :, dd : dd + 2 * PAIR, :].rearrange("p h (c w) t -> p c h (w t)", c=2)[:, :, :, 0:BLOCK],
                     op=ALU.mult,
                 )
-            for dd in range(1, V_DIAGS + 1):
+            nc.gpsimd.tensor_tensor(
+                out=kk_blocks[:, :, HALF - 1, 0 : HALF * PACK],
+                in0=kx[:, :, 0:HALF, :].rearrange("p h d t -> p h (d t)"),
+                in1=kx[:, :, HALF:D, :].rearrange("p h d t -> p h (d t)"),
+                op=ALU.mult,
+            )
+            for dd in range(1, V_DIAGS + 1, 2):
+                n = min(2, V_DIAGS + 1 - dd)
                 nc.vector.tensor_tensor(
-                    out=kk_blocks[:, :, dd - 1, :].rearrange("p h (d t) -> p h d t", t=PACK),
-                    in0=kn_hdt,
-                    in1=kx[:, :, dd : dd + D, :],
+                    out=kk_blocks[:, :, dd - 1 : dd - 1 + n, :].rearrange("p h c (d t) -> p c h d t", t=PACK),
+                    in0=kn_hdt.unsqueeze(1).to_broadcast([P, n, H, D, PACK]),
+                    in1=kx[:, :, dd : dd + n * PAIR, :].rearrange("p h (c w) t -> p c h w t", c=n)[:, :, :, 0:D, :],
                     op=ALU.mult,
                 )
 

@@ -23,11 +23,11 @@ K_PASS = P * PACK
 GROUPS = B * N_TOK // K_PASS
 HALF = D // 2
 N_DIAG = HALF + 1
-D_EXT = D + HALF
 K_EXT = 2 * D + HALF
 PAIR = D + 1
 N_BLOCKS = N_DIAG + 1
-A_PITCH = D_EXT
+SKEW = D + 1
+BACK = D - 1
 EPS = 1e-12
 SCALE = 32.0 ** 0.25
 GP_DIAGS = 5
@@ -109,9 +109,11 @@ def tile_taylorsoftmaxattention_pa_t_kernel(tc, x, Wk, bk, Wv, bv, out_0, out_1,
         knp = [const.tile([P, PACK, P + 4], F32, name="knp%d" % i) for i in range(4)]
         for t in knp:
             nc.vector.memset(t[:, :, P : P + 1], 1.0)
-        a_mat = [const.tile([P, D * (A_PITCH + 1)], F32, name="a_mat%d" % i) for i in range(2)]
-        for t in a_mat:
-            nc.vector.memset(t[:], 0.0)
+        full = [const.tile([P, (D + 1) * D], F32, name="full%d" % i, align_bytes=64) for i in range(2)]
+        over_low = const.tile([P, (HALF + 1) * D], F32, name="over_low")
+        over_up = const.tile([P, 2 * HALF * D], F32, name="over_up")
+        nc.vector.memset(over_low[:], 0.0)
+        nc.vector.memset(over_up[:], 0.0)
         kk = const.tile([P, H * N_BLOCKS * BLOCK], BF16, name="kk", align_bytes=64)
         kk_blocks = kk[:].rearrange("p (h a n) -> p h a n", h=H, a=N_BLOCKS)
         nc.vector.memset(kk_blocks[:, :, HALF - 1, :], 0.0)
@@ -308,17 +310,35 @@ def tile_taylorsoftmaxattention_pa_t_kernel(tc, x, Wk, bk, Wv, bv, out_0, out_1,
                         )
             state[("u", b)] = (u1, u2)
 
+        def skewed(tile, first, rows, count):
+            return tile[:, first : first + rows * SKEW].rearrange("p (r q) -> p r q", q=SKEW)[:, :, 0:count]
+
+        def backward(u1, first, rows, count):
+            return u1[:, first : first + count * BACK].rearrange("p (k r) -> p r k", r=BACK)[:, 0:rows, ::-1]
+
         def unskew(b):
             u1, u2 = state[("u", b)]
-            a_flat = a_mat[b % 2]
-            a_skew = a_flat[:].rearrange("p (i q) -> p i q", q=A_PITCH + 1)
-            a_rows = a_flat[:, 0 : D * A_PITCH].rearrange("p (r c) -> p r c", c=A_PITCH)
-            nc.scalar.copy(out=a_skew[:, :, 1 : HALF + 1], in_=u1[:].rearrange("p (a i) -> p i a", i=D))
-            nc.scalar.mul(out=a_skew[:, :, 0:1], in_=u2[:, 0:D].unsqueeze(2), mul=0.5)
+            whole = full[b % 2]
+            forward = u1[:].rearrange("p (a i) -> p i a", i=D)
+            nc.scalar.copy(out=skewed(over_low, 1, HALF, HALF), in_=forward[:, HALF:D, :])
+            nc.scalar.copy(out=skewed(over_up, HALF + 1, HALF - 1, HALF), in_=backward(u1, 0, HALF - 1, HALF))
+            nc.scalar.copy(
+                out=skewed(over_up, HALF * D + 1, HALF - 1, HALF - 1), in_=backward(u1, BACK, HALF - 1, HALF - 1)
+            )
+            copy = nc.vector.tensor_copy if b == B - 1 else nc.scalar.copy
+            copy(
+                out=whole[:, HALF * D : D * D].rearrange("p (r s c) -> p r s c", s=2, c=HALF),
+                in_=over_low[:, 0 : HALF * D].rearrange("p (r s c) -> p r s c", s=2, c=HALF)[:, :, ::-1, :],
+            )
+            copy(
+                out=whole[:, 0 : HALF * D].rearrange("p (r s c) -> p r s c", s=2, c=HALF),
+                in_=over_up[:].rearrange("p (s r c) -> p r s c", s=2, c=D)[:, :, :, 0:HALF],
+            )
+            nc.scalar.copy(out=skewed(whole, 1, HALF, HALF), in_=forward[:, 0:HALF, :])
+            nc.scalar.copy(out=skewed(whole, HALF * D, HALF, HALF), in_=backward(u1, HALF - 1, HALF, HALF))
+            nc.scalar.copy(out=skewed(whole, 0, D, 1), in_=u2[:, 0:D].unsqueeze(2))
             kv_sb = work.tile([P, D], F32, name="kv_sb", align_bytes=64)
             nc.scalar.copy(out=kv_sb[:], in_=u2[:, D : 2 * D])
-            nc.scalar.copy(out=a_rows[:, HALF:D, 0:HALF], in_=a_rows[:, HALF:D, D:D_EXT])
-            state[("a_rows", b)] = a_rows
             state[("kv_sb", b)] = kv_sb
 
         def plain_sums(b):
@@ -343,34 +363,24 @@ def tile_taylorsoftmaxattention_pa_t_kernel(tc, x, Wk, bk, Wv, bv, out_0, out_1,
             nc.scalar.mul(out=kvf[:, 0:1], in_=gram[:, P : P + 1], mul=1.0 / N_TOK)
             state[("fin", b)] = (fin, kvf)
 
-        def symmetrise(b):
-            a_rows = state[("a_rows", b)]
-            sym = work.tile([P, D * D], F32, name="sym", align_bytes=64)
-            nc.vector.tensor_tensor(
-                out=sym[:].rearrange("p (r c v) -> p c r v", r=D, v=4),
-                in0=a_rows[:, :, 0:D].rearrange("p r (c v) -> p c r v", v=4),
-                in1=a_rows[:, :, 0:D].rearrange("p (c v) r -> p c r v", v=4),
-                op=ALU.add,
-            )
-            state[("sym", b)] = sym
-
         def turn(b):
-            sym = state[("sym", b)]
-            turned = work.tile([P, D * D], F32, name="turned", align_bytes=64)
-            nc.vector.transpose(out=turned[:], in_=sym[:])
+            fin, kvf = state[("fin", b)]
             kv_turned = work.tile([P, D], F32, name="kv_turned", align_bytes=64)
             nc.vector.transpose(out=kv_turned[:], in_=state[("kv_sb", b)][:])
-            state[("turned", b)] = (turned, kv_turned)
-
-        def store(b):
-            fin, kvf = state[("fin", b)]
-            turned, kv_turned = state[("turned", b)]
-            nc.scalar.copy(out=fin[:, :, 1 : D + 1], in_=turned[:].rearrange("p (j e) -> p j e", e=D))
             nc.scalar.copy(out=kvf[:, 1 : D + 1], in_=kv_turned[:])
-            nc.scalar.dma_start(
-                out=out_0[b].rearrange("h i j e -> (h i) (j e)"), in_=fin[:].rearrange("p j e -> p (j e)")
-            )
             nc.scalar.dma_start(out=out_1[b].rearrange("h d e -> (h d) e"), in_=kvf[:])
+            turned = work.tile([P, D * D], F32, name="turned", align_bytes=64)
+            rows_out = out_0[b].rearrange("h i j e -> (h i) j e")
+            parts = 2 if b == B - 1 else 1
+            n = D // parts
+            for first in range(0, D, n):
+                words = slice(D * first, D * (first + n))
+                nc.vector.transpose(out=turned[:, words], in_=full[b % 2][:, words])
+                nc.scalar.copy(
+                    out=fin[:, first : first + n, 1 : D + 1],
+                    in_=turned[:, words].rearrange("p (j e) -> p j e", e=D),
+                )
+                nc.scalar.dma_start(out=rows_out[:, first : first + n, :], in_=fin[:, first : first + n, :])
 
         def value_sums():
             vs_pairs = vs_cols[:].rearrange("p (b j) -> p b j", j=2)
@@ -390,8 +400,6 @@ def tile_taylorsoftmaxattention_pa_t_kernel(tc, x, Wk, bk, Wv, bv, out_0, out_1,
             finishing = s >= 3 and s % 2 == 1
             if on(s):
                 mult(s)
-            if finishing:
-                symmetrise((s - 3) // 2)
             if on(s + 1):
                 norm_k(s + 1)
                 back_a(s + 1)
@@ -404,7 +412,6 @@ def tile_taylorsoftmaxattention_pa_t_kernel(tc, x, Wk, bk, Wv, bv, out_0, out_1,
                 project_b(s + 2)
             if closing:
                 stage2(s // 2 - 1)
-                unskew(s // 2 - 1)
                 plain_sums(s // 2 - 1)
             if on(s):
                 quant_v(s)
@@ -414,9 +421,9 @@ def tile_taylorsoftmaxattention_pa_t_kernel(tc, x, Wk, bk, Wv, bv, out_0, out_1,
                 turn((s - 3) // 2)
             if on(s + 3):
                 turn_x(s + 3)
+            if closing:
+                unskew(s // 2 - 1)
             if on(s + 6):
                 load_x(s + 6)
-            if finishing:
-                store((s - 3) // 2)
             if s == GROUPS - 2:
                 value_sums()

from contextlib import ExitStack

import concourse.mybir as mybir
from concourse.masks import make_identity

F32 = mybir.dt.float32
BF16 = mybir.dt.bfloat16
U32 = mybir.dt.uint32
U8 = mybir.dt.uint8
I32 = mybir.dt.int32
FP8X4 = mybir.dt.float8_e4m3fn_x4
ACT = mybir.ActivationFunctionType
ALU = mybir.AluOpType

P = 128
B = 8
N_TOK = 1024
C = 1024
H = 4
D = 32
PACK = 4
K_PASS = P * PACK
GROUPS = B * N_TOK // K_PASS
HALF = D // 2
N_DIAG = HALF + 1
K_EXT = 2 * D + HALF
PAIR = D + 1
N_BLOCKS = N_DIAG + 1
SKEW = D + 1
BACK = D - 1
EPS = 1e-12
SCALE = 32.0 ** 0.25
GP_DIAGS = 5
V_DIAGS = HALF - GP_DIAGS
BLOCK = D * PACK
HEAD_WORDS = N_BLOCKS * D
KK_WORDS = H * HEAD_WORDS
TAIL = 2 * D

FLOPS = 2 * B * N_TOK * C * 2 * H * D + 2 * B * H * N_TOK * (D * D + D) * D


def tile_taylorsoftmaxattention_pa_t_kernel(tc, x, Wk, bk, Wv, bv, out_0, out_1, out_2):
    nc = tc.nc
    with ExitStack() as ctx:
        const = ctx.enter_context(tc.tile_pool(name="const", bufs=1))
        xpool = ctx.enter_context(tc.tile_pool(name="xpool", bufs=3))
        work = ctx.enter_context(tc.tile_pool(name="work", bufs=2))
        keep = ctx.enter_context(tc.tile_pool(name="keep", bufs=4))
        ps_xt = ctx.enter_context(tc.psum_pool(name="ps_xt", bufs=3))
        ps_s1 = ctx.enter_context(tc.psum_pool(name="ps_s1", bufs=2))
        ps_kn = ctx.enter_context(tc.psum_pool(name="ps_kn", bufs=1))
        ps_misc = ctx.enter_context(tc.psum_pool(name="ps_misc", bufs=2))

        state = {}

        def load_x(g):
            b, gl = divmod(g, 2)
            x_sb = xpool.tile([P, PACK, C], BF16, name="x_sb")
            nc.sync.dma_start(
                out=x_sb[:],
                in_=x[b, K_PASS * gl : K_PASS * gl + K_PASS, :].rearrange("(p t) c -> p t c", t=PACK),
            )
            state[("x_sb", g)] = x_sb

        w_sb = const.tile([P, 2, C], BF16, name="w_sb")
        nc.sync.dma_start(out=w_sb[:, 0, :], in_=Wk)
        nc.sync.dma_start(out=w_sb[:, 1, :], in_=Wv)
        brow = const.tile([P, P], BF16, name="brow")
        nc.vector.memset(brow[:], 0.0)
        nc.sync.dma_start(out=brow[0:1, :], in_=bk.rearrange("(o f) -> o f", o=1))
        nc.sync.dma_start(out=brow[1:2, :], in_=bv.rearrange("(o f) -> o f", o=1))
        for g in range(3):
            load_x(g)
        ident = const.tile([P, P], F32, name="ident")
        make_identity(nc, ident[:])
        same_head = const.tile([P, P], F32, name="same_head")
        nc.vector.memset(same_head[:], 0.0)
        for h in range(H):
            nc.vector.memset(same_head[D * h : D * h + D, D * h : D * h + D], 1.0)

        wg = const.tile([P, 2 * 2 * P * PACK], BF16, name="wg", align_bytes=64)
        wg_f = wg[:].bitcast(F32).rearrange("p (g n u) -> p g n u", g=2, u=2)
        for g2 in range(2):
            wt = ps_xt.tile([P, 2, 2 * P], F32, name="wt", tag="xt")
            for u in range(2):
                for kv in range(2):
                    wb = 2 * g2 + u
                    nc.tensor.transpose(
                        out=wt[:, u, P * kv : P * kv + P],
                        in_=w_sb[:, kv, :].bitcast(F32)[:, P * wb : P * wb + P],
                        identity=ident[:],
                    )
            nc.vector.tensor_copy(out=wg_f[:, g2, :, :], in_=wt[:].rearrange("p u n -> p n u"))
        w_codes = const.tile([P, 2 * 2 * P], U32, name="w_codes", align_bytes=64)
        w_scales = const.tile([P, 2 * 2 * P], U8, name="w_scales", align_bytes=64)
        nc.vector.quantize_mx(out=w_codes[:].bitcast(FP8X4), scales=w_scales[:], in_=wg[:])

        brow_f = const.tile([P, P], F32, name="brow_f")
        nc.vector.tensor_copy(out=brow_f[:], in_=brow[:])
        bcol_ps = ps_misc.tile([P, P], F32, name="bcol_ps", tag="misc")
        nc.tensor.transpose(out=bcol_ps[:], in_=brow_f[:], identity=ident[:])
        bias = const.tile([P, 2], F32, name="bias")
        nc.vector.tensor_copy(out=bias[:, 0:1], in_=bcol_ps[:, 0:1])
        nc.vector.tensor_scalar(
            out=bias[:, 1:2], in0=bcol_ps[:, 1:2], scalar1=1.0 / N_TOK, scalar2=None, op0=ALU.mult
        )

        knp = [const.tile([P, PACK, P + 4], F32, name="knp%d" % i) for i in range(4)]
        for t in knp:
            nc.vector.memset(t[:, :, P : P + 1], 1.0)
        full = [const.tile([P, (D + 1) * D], F32, name="full%d" % i, align_bytes=64) for i in range(2)]
        over_low = const.tile([P, (HALF + 1) * D], F32, name="over_low")
        over_up = const.tile([P, 2 * HALF * D], F32, name="over_up")
        nc.vector.memset(over_low[:], 0.0)
        nc.vector.memset(over_up[:], 0.0)
        kk = const.tile([P, H * N_BLOCKS * BLOCK], BF16, name="kk", align_bytes=64)
        kk_blocks = kk[:].rearrange("p (h a n) -> p h a n", h=H, a=N_BLOCKS)
        nc.vector.memset(kk_blocks[:, :, HALF - 1, :], 0.0)
        kk_codes = [const.tile([P, KK_WORDS + TAIL], U32, name="kk_codes%d" % i, align_bytes=64) for i in range(4)]
        kk_scales = [const.tile([P, KK_WORDS + TAIL], U8, name="kk_scales%d" % i, align_bytes=64) for i in range(4)]
        for t in kk_codes + kk_scales:
            nc.vector.memset(t[:, KK_WORDS : KK_WORDS + TAIL], 0)
        v_masked = [const.tile([P, H * (P + D)], U32, name="v_masked%d" % i, align_bytes=64) for i in range(4)]
        for t in v_masked:
            nc.vector.memset(t[:], 0)
        vs_cols = const.tile([P, GROUPS], F32, name="vs_cols")
        vs_pad = const.tile([P, P], F32, name="vs_pad")
        nc.vector.memset(vs_pad[:], 0.0)
        vs_fin = const.tile([P, H, D + 1], F32, name="vs_fin")
        nc.vector.memset(vs_fin[:], 1.0)

        def turn_x(g):
            x_sb = state[("x_sb", g)]
            xg = work.tile([P, 2 * K_PASS * PACK], BF16, name="xg", align_bytes=64)
            xg_f = xg[:].bitcast(F32).rearrange("p (g n u) -> p g n u", g=2, u=2)
            for g2 in range(2):
                for th in range(2):
                    xt = ps_xt.tile([P, 2, 2 * P], F32, name="xt", tag="xt")
                    for u in range(2):
                        for tl in range(2):
                            wb = 2 * g2 + u
                            nc.tensor.transpose(
                                out=xt[:, u, P * tl : P * tl + P],
                                in_=x_sb[:, 2 * th + tl, :].bitcast(F32)[:, P * wb : P * wb + P],
                                identity=ident[:],
                            )
                    nc.scalar.copy(
                        out=xg_f[:, g2, 2 * P * th : 2 * P * th + 2 * P, :],
                        in_=xt[:].rearrange("p u n -> p n u"),
                    )
            state[("xg", g)] = xg

        def quant_x(g):
            x_codes = work.tile([P, 2 * K_PASS], U32, name="x_codes", align_bytes=64)
            x_scales = work.tile([P, 2 * K_PASS], U8, name="x_scales", align_bytes=64)
            nc.vector.quantize_mx(out=x_codes[:].bitcast(FP8X4), scales=x_scales[:], in_=state[("xg", g)][:])
            state[("xq", g)] = (x_codes, x_scales)

        def project_a(g):
            x_codes, x_scales = state[("xq", g)]
            proj = []
            for kv in range(2):
                acc = ps_s1.tile([P, K_PASS], F32, name="acc", tag="s1")
                for g2 in range(2):
                    wcols = slice(P * (2 * g2 + kv), P * (2 * g2 + kv) + P)
                    xcols = slice(K_PASS * g2, K_PASS * g2 + K_PASS)
                    nc.tensor.matmul_mx(
                        out=acc[:],
                        lhsT=w_codes[:, wcols].bitcast(FP8X4),
                        lhsT_scale=w_scales[:, wcols],
                        rhs=x_codes[:, xcols].bitcast(FP8X4),
                        rhs_scale=x_scales[:, xcols],
                        start=(g2 == 0),
                        stop=(g2 == 1),
                    )
                proj.append(acc)
            kT = work.tile([P, K_PASS], F32, name="kT")
            sqT = work.tile([P, K_PASS], F32, name="sqT")
            nc.scalar.activation(out=sqT[:], in_=proj[0][:], func=ACT.Square, bias=bias[:, 0:1], scale=1.0)
            nc.scalar.activation(out=kT[:], in_=proj[0][:], func=ACT.Identity, bias=bias[:, 0:1], scale=1.0)
            ssT = ps_s1.tile([P, K_PASS], F32, name="ssT", tag="s1")
            nc.tensor.matmul(out=ssT[:], lhsT=same_head[:], rhs=sqT[:], start=True, stop=True)
            state[("proj", g)] = (proj[1], kT, ssT)

        def project_b(g):
            acc_v, kT, ssT = state[("proj", g)]
            vT = work.tile([P, K_PASS], F32, name="vT")
            nc.scalar.activation(
                out=vT[:],
                in_=acc_v[:],
                func=ACT.Identity,
                bias=bias[:, 1:2],
                scale=1.0 / N_TOK,
                accum_out=vs_cols[:, g : g + 1],
            )
            rT = work.tile([P, K_PASS], F32, name="rT")
            nc.scalar.activation(out=rT[:], in_=ssT[:], func=ACT.Abs_reciprocal_sqrt, scale=1.0 / (SCALE * SCALE))
            state[("kr", g)] = (kT, rT)
            state[("vT", g)] = vT

        def norm_k(g):
            kT, rT = state[("kr", g)]
            knT = work.tile([P, K_PASS], F32, name="knT")
            nc.vector.scalar_tensor_tensor(
                out=knT[:], in0=rT[:], scalar=SCALE / EPS, in1=kT[:], op0=ALU.min, op1=ALU.mult
            )
            state[("knT", g)] = knT

        def back_a(g):
            knT = state[("knT", g)]
            kn_tok = ps_kn.tile([P, PACK, P], F32, name="kn_tok", tag="kn")
            for t in range(PACK):
                nc.tensor.transpose(out=kn_tok[:, t, :], in_=knT[:, P * t : P * t + P], identity=ident[:])
            kx = work.tile([P, H, K_EXT, PACK], F32, name="kx")
            nc.scalar.copy(
                out=kx[:, :, 0 : 2 * D, :].rearrange("p h (r d) t -> p r h d t", r=2),
                in_=kn_tok[:].rearrange("p t (h d) -> p h d t", h=H).unsqueeze(1).to_broadcast([P, 2, H, D, PACK]),
            )
            nc.scalar.copy(out=kx[:, :, 2 * D : K_EXT, :], in_=kx[:, :, 0:HALF, :])
            state[("kn_tok", g)] = kn_tok
            state[("kx", g)] = kx

        def back_b(g):
            vT = state[("vT", g)]
            kx = state[("kx", g)]
            v_tok = ps_misc.tile([P, PACK, P], F32, name="v_tok", tag="misc")
            for t in range(PACK):
                nc.tensor.transpose(out=v_tok[:, t, :], in_=vT[:, P * t : P * t + P], identity=ident[:])
            nc.scalar.copy(
                out=knp[g % 4][:, :, 0:P].rearrange("p t (h d) -> p h d t", h=H),
                in_=kx[:, :, 0:D, :],
            )
            vb = work.tile([P, K_PASS], BF16, name="vb", align_bytes=64)
            nc.scalar.copy(
                out=vb[:].rearrange("p (f t) -> p f t", t=PACK), in_=v_tok[:].rearrange("p t f -> p f t")
            )
            state[("vb", g)] = vb

        def quant_v(g):
            v_codes = keep.tile([P, P], U32, name="v_codes", align_bytes=64)
            v_scales = keep.tile([P, P], U8, name="v_scales", align_bytes=64)
            nc.vector.quantize_mx(out=v_codes[:].bitcast(FP8X4), scales=v_scales[:], in_=state[("vb", g)][:])
            state[("v", g)] = (v_codes, v_scales)

        def mask_v(g):
            v_codes, v_scales = state[("v", g)]
            nc.vector.tensor_copy(
                out=v_masked[g % 4][:].bitcast(I32).rearrange("p (h q) -> p h q", h=H)[:, :, 0:D],
                in_=v_codes[:].bitcast(I32).rearrange("p (h d) -> p h d", h=H),
            )

        def mult(g):
            kn_tok = state[("kn_tok", g)]
            kx = state[("kx", g)]
            kn_hdt = kn_tok[:].rearrange("p t (h d) -> p h d t", h=H)
            kx_flat = kx[:, :, 0:D, :].rearrange("p h d t -> p h (d t)")
            nc.scalar.activation(out=kk_blocks[:, :, HALF, :], in_=kx_flat, func=ACT.Square)
            nc.scalar.copy(out=kk_blocks[:, :, HALF + 1, :], in_=kx_flat)
            for dd in range(V_DIAGS + 1, HALF, 2):
                nc.gpsimd.tensor_tensor(
                    out=kk_blocks[:, :, dd - 1 : dd + 1, :].rearrange("p h c n -> p c h n"),
                    in0=kx_flat.unsqueeze(1).to_broadcast([P, 2, H, BLOCK]),
                    in1=kx[:, :, dd : dd + 2 * PAIR, :].rearrange("p h (c w) t -> p c h (w t)", c=2)[:, :, :, 0:BLOCK],
                    op=ALU.mult,
                )
            nc.gpsimd.tensor_tensor(
                out=kk_blocks[:, :, HALF - 1, 0 : HALF * PACK],
                in0=kx[:, :, 0:HALF, :].rearrange("p h d t -> p h (d t)"),
                in1=kx[:, :, HALF:D, :].rearrange("p h d t -> p h (d t)"),
                op=ALU.mult,
            )
            for dd in range(1, V_DIAGS + 1, 2):
                n = min(2, V_DIAGS + 1 - dd)
                nc.vector.tensor_tensor(
                    out=kk_blocks[:, :, dd - 1 : dd - 1 + n, :].rearrange("p h c (d t) -> p c h d t", t=PACK),
                    in0=kn_hdt.unsqueeze(1).to_broadcast([P, n, H, D, PACK]),
                    in1=kx[:, :, dd : dd + n * PAIR, :].rearrange("p h (c w) t -> p c h w t", c=n)[:, :, :, 0:D, :],
                    op=ALU.mult,
                )

        def quant_kk(g):
            done = 0
            for size in (4096, 4096, 1024):
                words = slice(done // PACK, (done + size) // PACK)
                nc.vector.quantize_mx(
                    out=kk_codes[g % 4][:, words].bitcast(FP8X4),
                    scales=kk_scales[g % 4][:, words],
                    in_=kk[:, done : done + size],
                )
                done += size

        def stage2(b):
            u1 = ps_misc.tile([P, K_PASS], F32, name="u1", tag="misc")
            u2 = ps_misc.tile([P, P], F32, name="u2", tag="misc")
            for j in range(2):
                g = 2 * b + j
                v_scales = state[("v", g)][1]
                for h in range(H):
                    for out, first, n in ((u1, 0, K_PASS), (u2, K_PASS, P)):
                        cols = slice(HEAD_WORDS * h + first, HEAD_WORDS * h + first + n)
                        nc.tensor.matmul_mx(
                            out=out[:],
                            lhsT=v_masked[g % 4][:, P * h : P * h + P].bitcast(FP8X4),
                            lhsT_scale=v_scales[:],
                            rhs=kk_codes[g % 4][:, cols].bitcast(FP8X4),
                            rhs_scale=kk_scales[g % 4][:, cols],
                            start=(j == 0 and h == 0),
                            stop=(j == 1 and h == H - 1),
                        )
            state[("u", b)] = (u1, u2)

        def skewed(tile, first, rows, count):
            return tile[:, first : first + rows * SKEW].rearrange("p (r q) -> p r q", q=SKEW)[:, :, 0:count]

        def backward(u1, first, rows, count):
            return u1[:, first : first + count * BACK].rearrange("p (k r) -> p r k", r=BACK)[:, 0:rows, ::-1]

        def unskew(b):
            u1, u2 = state[("u", b)]
            whole = full[b % 2]
            forward = u1[:].rearrange("p (a i) -> p i a", i=D)
            nc.scalar.copy(out=skewed(over_low, 1, HALF, HALF), in_=forward[:, HALF:D, :])
            nc.scalar.copy(out=skewed(over_up, HALF + 1, HALF - 1, HALF), in_=backward(u1, 0, HALF - 1, HALF))
            nc.scalar.copy(
                out=skewed(over_up, HALF * D + 1, HALF - 1, HALF - 1), in_=backward(u1, BACK, HALF - 1, HALF - 1)
            )
            copy = nc.vector.tensor_copy if b == B - 1 else nc.scalar.copy
            copy(
                out=whole[:, HALF * D : D * D].rearrange("p (r s c) -> p r s c", s=2, c=HALF),
                in_=over_low[:, 0 : HALF * D].rearrange("p (r s c) -> p r s c", s=2, c=HALF)[:, :, ::-1, :],
            )
            copy(
                out=whole[:, 0 : HALF * D].rearrange("p (r s c) -> p r s c", s=2, c=HALF),
                in_=over_up[:].rearrange("p (s r c) -> p r s c", s=2, c=D)[:, :, :, 0:HALF],
            )
            nc.scalar.copy(out=skewed(whole, 1, HALF, HALF), in_=forward[:, 0:HALF, :])
            nc.scalar.copy(out=skewed(whole, HALF * D, HALF, HALF), in_=backward(u1, HALF - 1, HALF, HALF))
            nc.scalar.copy(out=skewed(whole, 0, D, 1), in_=u2[:, 0:D].unsqueeze(2))
            kv_sb = work.tile([P, D], F32, name="kv_sb", align_bytes=64)
            nc.scalar.copy(out=kv_sb[:], in_=u2[:, D : 2 * D])
            state[("kv_sb", b)] = kv_sb

        def plain_sums(b):
            gram = ps_misc.tile([P, P + 1], F32, name="gram", tag="misc")
            for j in range(2):
                for t in range(PACK):
                    kn = knp[(2 * b + j) % 4]
                    nc.tensor.matmul(
                        out=gram[:],
                        lhsT=kn[:, t, 0:P],
                        rhs=kn[:, t, 0 : P + 1],
                        start=(j == 0 and t == 0),
                        stop=(j == 1 and t == PACK - 1),
                    )
            fin = work.tile([P, D, D + 1], F32, name="fin")
            kvf = work.tile([P, D + 1], F32, name="kvf")
            for h in range(H):
                rows = slice(D * h, D * h + D)
                nc.scalar.mul(
                    out=fin[rows, :, 0:1], in_=gram[rows, D * h : D * h + D].unsqueeze(2), mul=1.0 / N_TOK
                )
            nc.scalar.mul(out=kvf[:, 0:1], in_=gram[:, P : P + 1], mul=1.0 / N_TOK)
            state[("fin", b)] = (fin, kvf)

        def turn(b):
            fin, kvf = state[("fin", b)]
            kv_turned = work.tile([P, D], F32, name="kv_turned", align_bytes=64)
            nc.vector.transpose(out=kv_turned[:], in_=state[("kv_sb", b)][:])
            nc.scalar.copy(out=kvf[:, 1 : D + 1], in_=kv_turned[:])
            nc.scalar.dma_start(out=out_1[b].rearrange("h d e -> (h d) e"), in_=kvf[:])
            turned = work.tile([P, D * D], F32, name="turned", align_bytes=64)
            rows_out = out_0[b].rearrange("h i j e -> (h i) j e")
            parts = 2 if b == B - 1 else 1
            n = D // parts
            for first in range(0, D, n):
                words = slice(D * first, D * (first + n))
                nc.vector.transpose(out=turned[:, words], in_=full[b % 2][:, words])
                nc.scalar.copy(
                    out=fin[:, first : first + n, 1 : D + 1],
                    in_=turned[:, words].rearrange("p (j e) -> p j e", e=D),
                )
                nc.scalar.dma_start(out=rows_out[:, first : first + n, :], in_=fin[:, first : first + n, :])

        def value_sums():
            vs_pairs = vs_cols[:].rearrange("p (b j) -> p b j", j=2)
            nc.vector.tensor_tensor(out=vs_pad[:, 0:B], in0=vs_pairs[:, :, 0], in1=vs_pairs[:, :, 1], op=ALU.add)
            vs_ps = ps_misc.tile([P, P], F32, name="vs_ps", tag="misc")
            nc.tensor.transpose(out=vs_ps[:], in_=vs_pad[:], identity=ident[:])
            nc.vector.tensor_copy(out=vs_fin[:, :, 1 : D + 1], in_=vs_ps[:].rearrange("p (h e) -> p h e", h=H))
            nc.sync.dma_start(
                out=out_2.rearrange("b h o e -> b (h o e)"), in_=vs_fin[0:B, :, :].rearrange("p h e -> p (h e)")
            )

        def on(g):
            return 0 <= g < GROUPS

        for s in range(-3, GROUPS + 2):
            closing = s >= 2 and s % 2 == 0
            finishing = s >= 3 and s % 2 == 1
            if on(s):
                mult(s)
            if on(s + 1):
                norm_k(s + 1)
                back_a(s + 1)
            if on(s + 2):
                quant_x(s + 2)
                project_a(s + 2)
            if on(s + 1):
                back_b(s + 1)
            if on(s + 2):
                project_b(s + 2)
            if closing:
                stage2(s // 2 - 1)
                plain_sums(s // 2 - 1)
            if on(s):
                quant_v(s)
                quant_kk(s)
                mask_v(s)
            if finishing:
                turn((s - 3) // 2)
            if on(s + 3):
                turn_x(s + 3)
            if closing:
                unskew(s // 2 - 1)
            if on(s + 6):
                load_x(s + 6)
            if s == GROUPS - 2:
                value_sums()
